import numpy as np
import ml_dtypes


def mxq(x, axis, fmt="e4m3"):
    dtype, down = {"e4m3": (ml_dtypes.float8_e4m3fn, 7), "e5m2": (ml_dtypes.float8_e5m2, 14)}[fmt]
    v = np.moveaxis(np.asarray(x, np.float32).astype(ml_dtypes.bfloat16).astype(np.float64), axis, -1)
    blocks = v.reshape(v.shape[:-1] + (-1, 32))
    amax = np.abs(blocks).max(-1, keepdims=True)
    byte = np.maximum(np.where(amax > 0, np.frexp(amax)[1] - 1 + 127, 0) - down, 1)
    scale = np.exp2(byte - 127.0)
    codes = (blocks / scale).astype(np.float32).astype(dtype).astype(np.float64)
    return np.moveaxis((codes * scale).reshape(v.shape), -1, axis)


WIDE = False


def mx_kscale(k):
    if not WIDE:
        return np.ones(k)
    levels = np.array([10, -10, 5, -5, 0])
    a = np.random.permutation(np.resize(levels, k // 512 * 4)).reshape(k // 512, 4)
    idx = np.arange(k)
    return np.exp2(a[idx // 512, idx % 128 // 32])


BF16 = ml_dtypes.bfloat16


def bf(x):
    return np.asarray(x, np.float32).astype(BF16)


def f64(x):
    return np.asarray(x).astype(np.float64)


B, S, IN_F, OUT_F, SPLIT, SPLIT_R = 2, 512, 2048, 2048, 512, 512


def _draw_path(R):
    rn = np.random.standard_normal
    s, t = mx_kscale(IN_F), mx_kscale(R)
    keep = s == s.min()
    g = np.sqrt(IN_F / np.sum(keep * s * s))
    lv = np.unique(t)
    lev = lv[np.arange(OUT_F) % len(lv)]
    pick = t[None, :] == lev[:, None]
    c = np.sqrt(R / pick.sum(1)) / lev
    V = bf(np.where(keep, rn((R, IN_F)), 0.0))
    U = bf(np.where(pick, rn((OUT_F, R)), 0.0))
    v2 = bf(rn((1, IN_F)) * s)
    v1 = bf(rn((1, R)) / np.sqrt(IN_F) * g * t)
    u2 = bf(rn((1, R)))
    u1 = bf(rn((1, OUT_F)) / np.sqrt(R) * c)
    return V, U, v2, v1, u2, u1


def setup_inputs():
    rn = np.random.standard_normal
    x = bf(rn((B, S, IN_F)))
    V, U, v2, v1, u2, u1 = _draw_path(SPLIT)
    V_R, U_R, v2_R, v1_R, u2_R, u1_R = _draw_path(SPLIT_R)
    return {
        "x": x,
        "V": V, "U": U, "v2": v2, "v1": v1, "u2": u2, "u1": u1,
        "V_R": V_R, "U_R": U_R, "v2_R": v2_R, "v1_R": v1_R, "u2_R": u2_R, "u1_R": u1_R,
        "bias": bf(rn(OUT_F) * 0.5),
    }


def _path(x2, V, U, v2, v1, u2, u1):
    Vq = np.sign(V)
    Uq = np.sign(U)
    h = mxq(x2 * v2, 1, "e4m3") @ mxq(Vq.T, 0, "e4m3")
    h = h * (v1 * u2)
    return (mxq(h, 1, "e4m3") @ mxq(Uq.T, 0, "e4m3")) * u1


def reference(x, V, U, v2, v1, u2, u1, V_R, U_R, v2_R, v1_R, u2_R, u1_R, bias):
    x = f64(x)
    b, s, hidden = x.shape
    x2 = x.reshape(-1, hidden)
    y = _path(x2, f64(V), f64(U), f64(v2), f64(v1), f64(u2), f64(u1))
    y = y + _path(x2, f64(V_R), f64(U_R), f64(v2_R), f64(v1_R), f64(u2_R), f64(u1_R))
    y = y + f64(bias)
    return y.reshape(b, s, -1)

@@ -1,0 +1,247 @@
+from contextlib import ExitStack
+
+import concourse.mybir as mybir
+from concourse.masks import make_identity
+
+F32 = mybir.dt.float32
+BF16 = mybir.dt.bfloat16
+U32 = mybir.dt.uint32
+U8 = mybir.dt.uint8
+FP8X4 = mybir.dt.float8_e4m3fn_x4
+ACT = mybir.ActivationFunctionType
+ALU = mybir.AluOpType
+
+P = 128
+BANK = 512
+K_PASS = 512
+TOKENS = 1024
+IN_F = 2048
+RANK = 512
+OUT_F = 2048
+IN_PASSES = IN_F // K_PASS
+UNIT = 4096
+UNIT_WORDS = UNIT // 4
+HALF = 512
+
+FLOPS = 2 * (2 * TOKENS * IN_F * RANK + 2 * TOKENS * RANK * OUT_F)
+
+
+def as_words(grouped, b):
+    return grouped[:, 1024 * b : 1024 * (b + 1)].rearrange("p (n u e) -> p n u e", u=2, e=2)
+
+
+def k_onto_partitions(nc, psum_t, ident, raw, bank_step, block_step, evacuate):
+    words = raw[:].bitcast(F32)
+    for b in range(4):
+        bank = psum_t.tile([P, BANK], F32, tag="t")
+        for u in range(2):
+            for s in range(2):
+                first = b * bank_step + s * block_step + P * u
+                nc.tensor.transpose(
+                    bank[:, 256 * u + P * s : 256 * u + P * (s + 1)], words[:, first : first + P], ident[:]
+                )
+        evacuate(b, bank[:].bitcast(BF16).rearrange("p (u n e) -> p n u e", u=2, e=2))
+
+
+def tile_littlebititqspeclinear_pa_kernel(
+    tc, x, V, U, v2, v1, u2, u1, V_R, U_R, v2_R, v1_R, u2_R, u1_R, bias, out
+):
+    nc = tc.nc
+    x2 = x.flatten_outer_dims()
+    out2 = out.flatten_outer_dims()
+    with ExitStack() as ctx:
+        consts = ctx.enter_context(tc.tile_pool(name="consts", bufs=1))
+        keep = ctx.enter_context(tc.tile_pool(name="keep", bufs=1))
+        raws = ctx.enter_context(tc.tile_pool(name="raws", bufs=6))
+        groups = ctx.enter_context(tc.tile_pool(name="groups", bufs=2))
+        results = ctx.enter_context(tc.tile_pool(name="results", bufs=2))
+        psum_t = ctx.enter_context(tc.psum_pool(name="psum_t", bufs=3))
+        psum_mx = ctx.enter_context(tc.psum_pool(name="psum_mx", bufs=5))
+
+        ident = consts.tile([P, P], F32)
+        make_identity(nc, ident[:])
+
+        by_k_rows = consts.tile([P, 256], BF16)
+        nc.vector.memset(by_k_rows[:], 0.0)
+        first_row = 0
+        for vec in (v2, v2_R, v1, u2, v1_R, u2_R):
+            rows = vec.shape[1] // 256
+            nc.scalar.dma_start(
+                out=by_k_rows[first_row : first_row + rows, :], in_=vec.rearrange("o (r c) -> (o r) c", c=256)
+            )
+            first_row += rows
+        by_k_bank = psum_t.tile([P, BANK], F32, tag="t")
+        nc.tensor.transpose(by_k_bank[:, 0:P], by_k_rows[:].bitcast(F32), ident[:])
+        by_k = consts.tile([P, 2 * first_row], F32)
+        nc.vector.tensor_copy(out=by_k[:], in_=by_k_bank[:].bitcast(BF16)[:, 0 : 2 * first_row])
+        v2_cols = (0, 16)
+        rank_scale = consts.tile([P, 2, 4], F32)
+        for path in range(2):
+            nc.vector.tensor_tensor(
+                out=rank_scale[:, path, :],
+                in0=by_k[:, 32 + 8 * path : 36 + 8 * path],
+                in1=by_k[:, 36 + 8 * path : 40 + 8 * path],
+                op=ALU.mult,
+            )
+
+        by_o_rows = consts.tile([P, P], BF16)
+        nc.vector.memset(by_o_rows[:], 0.0)
+        o_tiles = OUT_F // P
+        for i, vec in enumerate((u1.rearrange("o f -> (o f)"), u1_R.rearrange("o f -> (o f)"), bias)):
+            nc.scalar.dma_start(
+                out=by_o_rows[o_tiles * i : o_tiles * (i + 1), :], in_=vec.rearrange("(r c) -> r c", c=P)
+            )
+        by_o_rows32 = consts.tile([P, P], F32)
+        nc.vector.tensor_copy(out=by_o_rows32[:], in_=by_o_rows[:])
+        by_o_bank = psum_t.tile([P, BANK], F32, tag="t")
+        nc.tensor.transpose(by_o_bank[:, 0:P], by_o_rows32[:], ident[:])
+        by_o = consts.tile([P, 3 * o_tiles], F32)
+        nc.vector.tensor_copy(out=by_o[:], in_=by_o_bank[:, 0 : 3 * o_tiles])
+
+        def mx_operand(name, columns):
+            codes = [keep.tile([P, columns], U32, name="%s_codes%d" % (name, i), align_bytes=64) for i in range(2)]
+            scales = [keep.tile([P, columns], U8, name="%s_scales%d" % (name, i), align_bytes=64) for i in range(2)]
+            return codes, scales
+
+        x_codes, x_scales = mx_operand("x", IN_PASSES * TOKENS)
+        v_codes, v_scales = mx_operand("v", IN_PASSES * RANK)
+        u_codes, u_scales = mx_operand("u", OUT_F)
+        h_codes, h_scales = mx_operand("h", TOKENS)
+
+        def quantise(grouped, codes, scales, first, columns):
+            nc.vector.quantize_mx(
+                out=codes[:, first : first + columns].bitcast(FP8X4),
+                scales=scales[:, first : first + columns],
+                in_=grouped[:],
+            )
+
+        def sign_unit(rows_view, bank_step, block_step, codes, scales, first):
+            raw = raws.tile([P, UNIT], BF16, tag="raw")
+            nc.sync.dma_start(out=raw[:].rearrange("p (a c) -> p a c", a=rows_view.shape[1]), in_=rows_view)
+            signs = groups.tile([P, UNIT], BF16, tag="signs", align_bytes=64)
+
+            def evacuate(b, values):
+                nc.scalar.activation(out=as_words(signs, b), in_=values, func=ACT.Sign)
+
+            k_onto_partitions(nc, psum_t, ident, raw, bank_step, block_step, evacuate)
+            quantise(signs, codes, scales, first, UNIT_WORDS)
+
+        def v_unit(path, pair):
+            rows = (V, V_R)[path][256 * pair : 256 * (pair + 1), :].rearrange("(j s) k -> j s k", s=2)
+            sign_unit(rows, 256, 1024, v_codes[path], v_scales[path], UNIT_WORDS * pair)
+
+        def u_unit(path, part):
+            rows = (U, U_R)[path][1024 * part : 1024 * (part + 1), :].rearrange("(a j) r -> j a r", j=P)
+            sign_unit(rows, 512, 256, u_codes[path], u_scales[path], UNIT_WORDS * part)
+
+        def x_unit(pair):
+            raw = raws.tile([P, UNIT], BF16, tag="raw")
+            nc.sync.dma_start(
+                out=raw[:].rearrange("p (s k) -> p s k", s=2),
+                in_=x2[256 * pair : 256 * (pair + 1), :].rearrange("(s p) k -> p s k", p=P),
+            )
+            scaled = [groups.tile([P, UNIT], BF16, name="scaled%d" % path, tag="scaled%d" % path, align_bytes=64) for path in range(2)]
+
+            def evacuate(b, values):
+                for path in range(2):
+                    v2_of_pass = by_k[:, v2_cols[path] + 4 * b : v2_cols[path] + 4 * (b + 1)]
+                    nc.vector.tensor_tensor(
+                        out=as_words(scaled[path], b),
+                        in0=values,
+                        in1=v2_of_pass.rearrange("p (u e) -> p u e", u=2).unsqueeze(1).to_broadcast([P, 256, 2, 2]),
+                        op=ALU.mult,
+                    )
+
+            k_onto_partitions(nc, psum_t, ident, raw, 256, 1024, evacuate)
+            for path in range(2):
+                quantise(scaled[path], x_codes[path], x_scales[path], UNIT_WORDS * pair, UNIT_WORDS)
+
+        def first_matmul(half):
+            for path in range(2):
+                h_scaled = groups.tile([P, 4 * HALF], BF16, tag="h_scaled", align_bytes=64)
+                for i in range(HALF // P):
+                    token_tile = (HALF // P) * half + i
+                    tokens = UNIT_WORDS * (token_tile // 2) + P * (token_tile % 2)
+                    h_bank = psum_mx.tile([P, BANK], F32, tag="mx")
+                    for t in range(4):
+                        ranks = UNIT_WORDS * (t // 2) + P * (t % 2)
+                        for c in range(IN_PASSES):
+                            nc.tensor.matmul_mx(
+                                out=h_bank[:, P * t : P * (t + 1)],
+                                lhsT=v_codes[path][:, ranks + 256 * c : ranks + 256 * c + P].bitcast(FP8X4),
+                                lhsT_scale=v_scales[path][:, ranks + 256 * c : ranks + 256 * c + P],
+                                rhs=x_codes[path][:, tokens + 256 * c : tokens + 256 * c + P].bitcast(FP8X4),
+                                rhs_scale=x_scales[path][:, tokens + 256 * c : tokens + 256 * c + P],
+                                start=(c == 0),
+                                stop=(c == IN_PASSES - 1),
+                            )
+                    nc.vector.tensor_tensor(
+                        out=h_scaled[:, 4 * P * i : 4 * P * (i + 1)].rearrange("p (n t) -> p n t", t=4),
+                        in0=h_bank[:].rearrange("p (t n) -> p n t", t=4),
+                        in1=rank_scale[:, path, :].unsqueeze(1).to_broadcast([P, P, 4]),
+                        op=ALU.mult,
+                    )
+                quantise(h_scaled, h_codes[path], h_scales[path], HALF * half, HALF)
+
+        def second_matmul(half):
+            tokens = slice(HALF * half, HALF * (half + 1))
+            for o_group in range(OUT_F // BANK):
+                y_t = []
+                for a in range(4 * o_group, 4 * (o_group + 1)):
+                    features = slice(P * a, P * (a + 1))
+                    sums = []
+                    for path in range(2):
+                        acc = psum_mx.tile([P, BANK], F32, tag="mx", name="acc%d" % path)
+                        nc.tensor.matmul_mx(
+                            out=acc[:],
+                            lhsT=u_codes[path][:, features].bitcast(FP8X4),
+                            lhsT_scale=u_scales[path][:, features],
+                            rhs=h_codes[path][:, tokens].bitcast(FP8X4),
+                            rhs_scale=h_scales[path][:, tokens],
+                            start=True,
+                            stop=True,
+                        )
+                        sums.append(acc)
+                    primary = results.tile([P, HALF], F32, tag="primary")
+                    nc.scalar.activation(
+                        out=primary[:],
+                        in_=sums[0][:],
+                        func=ACT.Identity,
+                        scale=by_o[:, a : a + 1],
+                        bias=by_o[:, 2 * o_tiles + a : 2 * o_tiles + a + 1],
+                    )
+                    both = results.tile([P, HALF], F32, tag="both", bufs=8)
+                    nc.vector.scalar_tensor_tensor(
+                        out=both[:],
+                        in0=sums[1][:],
+                        scalar=by_o[:, o_tiles + a : o_tiles + a + 1],
+                        in1=primary[:],
+                        op0=ALU.mult,
+                        op1=ALU.add,
+                    )
+                    y_t.append(both)
+                for i in range(HALF // P):
+                    y_bank = psum_t.tile([P, BANK], F32, tag="t")
+                    for j in range(4):
+                        nc.tensor.transpose(y_bank[:, P * j : P * (j + 1)], y_t[j][:, P * i : P * (i + 1)], ident[:])
+                    y = results.tile([P, BANK], F32, tag="y", bufs=3)
+                    nc.scalar.copy(out=y[:], in_=y_bank[:])
+                    first_token = HALF * half + P * i
+                    nc.sync.dma_start(
+                        out=out2[first_token : first_token + P, BANK * o_group : BANK * (o_group + 1)], in_=y[:]
+                    )
+
+        for path in range(2):
+            for pair in range(2):
+                v_unit(path, pair)
+        x_unit(0)
+        x_unit(1)
+        first_matmul(0)
+        for path in range(2):
+            for part in range(2):
+                u_unit(path, part)
+        second_matmul(0)
+        x_unit(2)
+        x_unit(3)
+        first_matmul(1)
+        second_matmul(1)

@@ -22,25 +22,13 @@ IN_PASSES = IN_F // K_PASS
 UNIT = 4096
 UNIT_WORDS = UNIT // 4
 HALF = 512
+ALL_BANKS = (0, 1, 2, 3)
 
 FLOPS = 2 * (2 * TOKENS * IN_F * RANK + 2 * TOKENS * RANK * OUT_F)
 
 
 def as_words(grouped, b):
     return grouped[:, 1024 * b : 1024 * (b + 1)].rearrange("p (n u e) -> p n u e", u=2, e=2)
-
-
-def k_onto_partitions(nc, psum_t, ident, raw, bank_step, block_step, evacuate):
-    words = raw[:].bitcast(F32)
-    for b in range(4):
-        bank = psum_t.tile([P, BANK], F32, tag="t")
-        for u in range(2):
-            for s in range(2):
-                first = b * bank_step + s * block_step + P * u
-                nc.tensor.transpose(
-                    bank[:, 256 * u + P * s : 256 * u + P * (s + 1)], words[:, first : first + P], ident[:]
-                )
-        evacuate(b, bank[:].bitcast(BF16).rearrange("p (u n e) -> p n u e", u=2, e=2))
 
 
 def tile_littlebititqspeclinear_pa_kernel(
@@ -53,50 +41,11 @@ def tile_littlebititqspeclinear_pa_kernel(
         consts = ctx.enter_context(tc.tile_pool(name="consts", bufs=1))
         keep = ctx.enter_context(tc.tile_pool(name="keep", bufs=1))
         raws = ctx.enter_context(tc.tile_pool(name="raws", bufs=6))
-        groups = ctx.enter_context(tc.tile_pool(name="groups", bufs=2))
-        results = ctx.enter_context(tc.tile_pool(name="results", bufs=2))
-        psum_t = ctx.enter_context(tc.psum_pool(name="psum_t", bufs=3))
-        psum_mx = ctx.enter_context(tc.psum_pool(name="psum_mx", bufs=5))
-
-        ident = consts.tile([P, P], F32)
-        make_identity(nc, ident[:])
-
-        by_k_rows = consts.tile([P, 256], BF16)
-        nc.vector.memset(by_k_rows[:], 0.0)
-        first_row = 0
-        for vec in (v2, v2_R, v1, u2, v1_R, u2_R):
-            rows = vec.shape[1] // 256
-            nc.scalar.dma_start(
-                out=by_k_rows[first_row : first_row + rows, :], in_=vec.rearrange("o (r c) -> (o r) c", c=256)
-            )
-            first_row += rows
-        by_k_bank = psum_t.tile([P, BANK], F32, tag="t")
-        nc.tensor.transpose(by_k_bank[:, 0:P], by_k_rows[:].bitcast(F32), ident[:])
-        by_k = consts.tile([P, 2 * first_row], F32)
-        nc.vector.tensor_copy(out=by_k[:], in_=by_k_bank[:].bitcast(BF16)[:, 0 : 2 * first_row])
-        v2_cols = (0, 16)
-        rank_scale = consts.tile([P, 2, 4], F32)
-        for path in range(2):
-            nc.vector.tensor_tensor(
-                out=rank_scale[:, path, :],
-                in0=by_k[:, 32 + 8 * path : 36 + 8 * path],
-                in1=by_k[:, 36 + 8 * path : 40 + 8 * path],
-                op=ALU.mult,
-            )
-
-        by_o_rows = consts.tile([P, P], BF16)
-        nc.vector.memset(by_o_rows[:], 0.0)
-        o_tiles = OUT_F // P
-        for i, vec in enumerate((u1.rearrange("o f -> (o f)"), u1_R.rearrange("o f -> (o f)"), bias)):
-            nc.scalar.dma_start(
-                out=by_o_rows[o_tiles * i : o_tiles * (i + 1), :], in_=vec.rearrange("(r c) -> r c", c=P)
-            )
-        by_o_rows32 = consts.tile([P, P], F32)
-        nc.vector.tensor_copy(out=by_o_rows32[:], in_=by_o_rows[:])
-        by_o_bank = psum_t.tile([P, BANK], F32, tag="t")
-        nc.tensor.transpose(by_o_bank[:, 0:P], by_o_rows32[:], ident[:])
-        by_o = consts.tile([P, 3 * o_tiles], F32)
-        nc.vector.tensor_copy(out=by_o[:], in_=by_o_bank[:, 0 : 3 * o_tiles])
+        groups = ctx.enter_context(tc.tile_pool(name="groups", bufs=1))
+        results = ctx.enter_context(tc.tile_pool(name="results", bufs=4))
+        psum_s = ctx.enter_context(tc.psum_pool(name="psum_s", bufs=4))
+        psum_v = ctx.enter_context(tc.psum_pool(name="psum_v", bufs=4))
+        ctx.enter_context(tc.manual_schedule())
 
         def mx_operand(name, columns):
             codes = [keep.tile([P, columns], U32, name="%s_codes%d" % (name, i), align_bytes=64) for i in range(2)]
@@ -115,133 +64,271 @@ def tile_littlebititqspeclinear_pa_kernel(
                 in_=grouped[:],
             )
 
-        def sign_unit(rows_view, bank_step, block_step, codes, scales, first):
+        ident = consts.tile([P, P], F32)
+        make_identity(nc, ident[:])
+
+        def load(rows, halve_columns):
             raw = raws.tile([P, UNIT], BF16, tag="raw")
-            nc.sync.dma_start(out=raw[:].rearrange("p (a c) -> p a c", a=rows_view.shape[1]), in_=rows_view)
-            signs = groups.tile([P, UNIT], BF16, tag="signs", align_bytes=64)
+            blocks, columns = rows.shape[1], rows.shape[2]
+            view = raw[:].rearrange("p (a c) -> p a c", a=blocks)
+            for half in range(2):
+                if halve_columns:
+                    part = slice(half * columns // 2, (half + 1) * columns // 2)
+                    nc.sync.dma_start(out=view[:, :, part], in_=rows[:, :, part])
+                else:
+                    part = slice(half * blocks // 2, (half + 1) * blocks // 2)
+                    nc.sync.dma_start(out=view[:, part, :], in_=rows[:, part, :])
+            return raw
 
-            def evacuate(b, values):
-                nc.scalar.activation(out=as_words(signs, b), in_=values, func=ACT.Sign)
+        def transposed_bank(psum, unit, b):
+            words = unit["raw"][:].bitcast(F32)
+            bank = psum.tile([P, BANK], F32, tag="bank")
+            for u in range(2):
+                for s in range(2):
+                    first = b * unit["bank_step"] + s * unit["block_step"] + P * u
+                    nc.tensor.transpose(
+                        bank[:, 256 * u + P * s : 256 * u + P * (s + 1)], words[:, first : first + P], ident[:]
+                    )
+            return bank[:].bitcast(BF16).rearrange("p (u n e) -> p n u e", u=2, e=2)
 
-            k_onto_partitions(nc, psum_t, ident, raw, bank_step, block_step, evacuate)
-            quantise(signs, codes, scales, first, UNIT_WORDS)
-
-        def v_unit(path, pair):
+        def open_v(path, pair):
             rows = (V, V_R)[path][256 * pair : 256 * (pair + 1), :].rearrange("(j s) k -> j s k", s=2)
-            sign_unit(rows, 256, 1024, v_codes[path], v_scales[path], UNIT_WORDS * pair)
+            return {
+                "raw": load(rows, True), "bank_step": 256, "block_step": 1024,
+                "codes": v_codes[path], "scales": v_scales[path], "first": UNIT_WORDS * pair,
+            }
 
-        def u_unit(path, part):
+        def open_u(path, part):
             rows = (U, U_R)[path][1024 * part : 1024 * (part + 1), :].rearrange("(a j) r -> j a r", j=P)
-            sign_unit(rows, 512, 256, u_codes[path], u_scales[path], UNIT_WORDS * part)
+            return {
+                "raw": load(rows, False), "bank_step": 512, "block_step": 256,
+                "codes": u_codes[path], "scales": u_scales[path], "first": UNIT_WORDS * part,
+            }
 
-        def x_unit(pair):
-            raw = raws.tile([P, UNIT], BF16, tag="raw")
-            nc.sync.dma_start(
-                out=raw[:].rearrange("p (s k) -> p s k", s=2),
-                in_=x2[256 * pair : 256 * (pair + 1), :].rearrange("(s p) k -> p s k", p=P),
-            )
-            scaled = [groups.tile([P, UNIT], BF16, name="scaled%d" % path, tag="scaled%d" % path, align_bytes=64) for path in range(2)]
+        def open_x(pair):
+            rows = x2[256 * pair : 256 * (pair + 1), :].rearrange("(s p) k -> p s k", p=P)
+            return {"raw": load(rows, True), "bank_step": 256, "block_step": 1024, "first": UNIT_WORDS * pair}
 
-            def evacuate(b, values):
+        def sign_banks(unit, banks):
+            for b in banks:
+                if b == 0:
+                    unit["signs"] = groups.tile([P, UNIT], BF16, name="signs", tag="signs", bufs=4, align_bytes=64)
+                values = transposed_bank(psum_s, unit, b)
+                nc.scalar.activation(out=as_words(unit["signs"], b), in_=values, func=ACT.Sign)
+
+        def close_signs(unit):
+            quantise(unit["signs"], unit["codes"], unit["scales"], unit["first"], UNIT_WORDS)
+
+        def x_banks(unit, banks):
+            for b in banks:
+                if b == 0:
+                    unit["scaled"] = [
+                        groups.tile([P, UNIT], BF16, name="scaled%d" % path, tag="scaled%d" % path, align_bytes=64)
+                        for path in range(2)
+                    ]
+                values = transposed_bank(psum_v, unit, b)
                 for path in range(2):
                     v2_of_pass = by_k[:, v2_cols[path] + 4 * b : v2_cols[path] + 4 * (b + 1)]
                     nc.vector.tensor_tensor(
-                        out=as_words(scaled[path], b),
+                        out=as_words(unit["scaled"][path], b),
                         in0=values,
                         in1=v2_of_pass.rearrange("p (u e) -> p u e", u=2).unsqueeze(1).to_broadcast([P, 256, 2, 2]),
                         op=ALU.mult,
                     )
 
-            k_onto_partitions(nc, psum_t, ident, raw, 256, 1024, evacuate)
+        def close_x(unit):
             for path in range(2):
-                quantise(scaled[path], x_codes[path], x_scales[path], UNIT_WORDS * pair, UNIT_WORDS)
+                quantise(unit["scaled"][path], x_codes[path], x_scales[path], unit["first"], UNIT_WORDS)
 
-        def first_matmul(half):
-            for path in range(2):
-                h_scaled = groups.tile([P, 4 * HALF], BF16, tag="h_scaled", align_bytes=64)
-                for i in range(HALF // P):
-                    token_tile = (HALF // P) * half + i
-                    tokens = UNIT_WORDS * (token_tile // 2) + P * (token_tile % 2)
-                    h_bank = psum_mx.tile([P, BANK], F32, tag="mx")
-                    for t in range(4):
-                        ranks = UNIT_WORDS * (t // 2) + P * (t % 2)
-                        for c in range(IN_PASSES):
-                            nc.tensor.matmul_mx(
-                                out=h_bank[:, P * t : P * (t + 1)],
-                                lhsT=v_codes[path][:, ranks + 256 * c : ranks + 256 * c + P].bitcast(FP8X4),
-                                lhsT_scale=v_scales[path][:, ranks + 256 * c : ranks + 256 * c + P],
-                                rhs=x_codes[path][:, tokens + 256 * c : tokens + 256 * c + P].bitcast(FP8X4),
-                                rhs_scale=x_scales[path][:, tokens + 256 * c : tokens + 256 * c + P],
-                                start=(c == 0),
-                                stop=(c == IN_PASSES - 1),
-                            )
-                    nc.vector.tensor_tensor(
-                        out=h_scaled[:, 4 * P * i : 4 * P * (i + 1)].rearrange("p (n t) -> p n t", t=4),
-                        in0=h_bank[:].rearrange("p (t n) -> p n t", t=4),
-                        in1=rank_scale[:, path, :].unsqueeze(1).to_broadcast([P, P, 4]),
-                        op=ALU.mult,
+        h_scaled = [None, None]
+
+        def first_matmul(token_tiles, path):
+            for token_tile in token_tiles:
+                i = token_tile % (HALF // P)
+                if i == 0:
+                    h_scaled[path] = groups.tile(
+                        [P, 4 * HALF], BF16, name="h_scaled%d" % path, tag="h_scaled%d" % path, align_bytes=64
                     )
-                quantise(h_scaled, h_codes[path], h_scales[path], HALF * half, HALF)
-
-        def second_matmul(half):
-            tokens = slice(HALF * half, HALF * (half + 1))
-            for o_group in range(OUT_F // BANK):
-                y_t = []
-                for a in range(4 * o_group, 4 * (o_group + 1)):
-                    features = slice(P * a, P * (a + 1))
-                    sums = []
-                    for path in range(2):
-                        acc = psum_mx.tile([P, BANK], F32, tag="mx", name="acc%d" % path)
+                tokens = UNIT_WORDS * (token_tile // 2) + P * (token_tile % 2)
+                h_bank = psum_v.tile([P, BANK], F32, tag="bank")
+                for t in range(4):
+                    ranks = UNIT_WORDS * (t // 2) + P * (t % 2)
+                    for c in range(IN_PASSES):
                         nc.tensor.matmul_mx(
-                            out=acc[:],
-                            lhsT=u_codes[path][:, features].bitcast(FP8X4),
-                            lhsT_scale=u_scales[path][:, features],
-                            rhs=h_codes[path][:, tokens].bitcast(FP8X4),
-                            rhs_scale=h_scales[path][:, tokens],
-                            start=True,
-                            stop=True,
+                            out=h_bank[:, P * t : P * (t + 1)],
+                            lhsT=v_codes[path][:, ranks + 256 * c : ranks + 256 * c + P].bitcast(FP8X4),
+                            lhsT_scale=v_scales[path][:, ranks + 256 * c : ranks + 256 * c + P],
+                            rhs=x_codes[path][:, tokens + 256 * c : tokens + 256 * c + P].bitcast(FP8X4),
+                            rhs_scale=x_scales[path][:, tokens + 256 * c : tokens + 256 * c + P],
+                            start=(c == 0),
+                            stop=(c == IN_PASSES - 1),
                         )
-                        sums.append(acc)
-                    primary = results.tile([P, HALF], F32, tag="primary")
-                    nc.scalar.activation(
-                        out=primary[:],
-                        in_=sums[0][:],
-                        func=ACT.Identity,
-                        scale=by_o[:, a : a + 1],
-                        bias=by_o[:, 2 * o_tiles + a : 2 * o_tiles + a + 1],
+                nc.vector.tensor_tensor(
+                    out=h_scaled[path][:, 4 * P * i : 4 * P * (i + 1)].rearrange("p (n t) -> p n t", t=4),
+                    in0=h_bank[:].rearrange("p (t n) -> p n t", t=4),
+                    in1=rank_scale[:, path, :].unsqueeze(1).to_broadcast([P, P, 4]),
+                    op=ALU.mult,
+                )
+
+        def close_h(path, half):
+            quantise(h_scaled[path], h_codes[path], h_scales[path], HALF * half, HALF)
+
+        def second_matmul(half, o_group):
+            tokens = slice(HALF * half, HALF * (half + 1))
+            y_t = []
+            for a in range(4 * o_group, 4 * (o_group + 1)):
+                features = slice(P * a, P * (a + 1))
+                sums = []
+                for path in range(2):
+                    acc = (psum_s, psum_v)[path].tile([P, BANK], F32, tag="bank", name="acc%d" % path)
+                    nc.tensor.matmul_mx(
+                        out=acc[:],
+                        lhsT=u_codes[path][:, features].bitcast(FP8X4),
+                        lhsT_scale=u_scales[path][:, features],
+                        rhs=h_codes[path][:, tokens].bitcast(FP8X4),
+                        rhs_scale=h_scales[path][:, tokens],
+                        start=True,
+                        stop=True,
                     )
-                    both = results.tile([P, HALF], F32, tag="both", bufs=8)
-                    nc.vector.scalar_tensor_tensor(
-                        out=both[:],
-                        in0=sums[1][:],
-                        scalar=by_o[:, o_tiles + a : o_tiles + a + 1],
-                        in1=primary[:],
-                        op0=ALU.mult,
-                        op1=ALU.add,
-                    )
-                    y_t.append(both)
-                for i in range(HALF // P):
-                    y_bank = psum_t.tile([P, BANK], F32, tag="t")
-                    for j in range(4):
-                        nc.tensor.transpose(y_bank[:, P * j : P * (j + 1)], y_t[j][:, P * i : P * (i + 1)], ident[:])
-                    y = results.tile([P, BANK], F32, tag="y", bufs=3)
+                    sums.append(acc)
+                primary = results.tile([P, HALF], F32, tag="primary")
+                nc.scalar.activation(
+                    out=primary[:],
+                    in_=sums[0][:],
+                    func=ACT.Identity,
+                    scale=by_o[:, a : a + 1],
+                    bias=by_o[:, 2 * o_tiles + a : 2 * o_tiles + a + 1],
+                )
+                both = results.tile([P, HALF], F32, tag="both", bufs=8)
+                nc.vector.scalar_tensor_tensor(
+                    out=both[:],
+                    in0=sums[1][:],
+                    scalar=by_o[:, o_tiles + a : o_tiles + a + 1],
+                    in1=primary[:],
+                    op0=ALU.mult,
+                    op1=ALU.add,
+                )
+                y_t.append(both)
+            return y_t
+
+        def store(half, o_group, y_t):
+            for i in range(HALF // P):
+                by_vector = half == 1 and i % 2 == 1
+                y_bank = (psum_v if by_vector else psum_s).tile([P, BANK], F32, tag="bank", name="y_bank")
+                for j in range(4):
+                    nc.tensor.transpose(y_bank[:, P * j : P * (j + 1)], y_t[j][:, P * i : P * (i + 1)], ident[:])
+                y = results.tile([P, BANK], F32, tag="y")
+                if by_vector:
+                    nc.vector.tensor_copy(out=y[:], in_=y_bank[:])
+                else:
                     nc.scalar.copy(out=y[:], in_=y_bank[:])
-                    first_token = HALF * half + P * i
-                    nc.sync.dma_start(
-                        out=out2[first_token : first_token + P, BANK * o_group : BANK * (o_group + 1)], in_=y[:]
-                    )
+                first_token = HALF * half + P * i
+                nc.sync.dma_start(
+                    out=out2[first_token : first_token + P, BANK * o_group : BANK * (o_group + 1)], in_=y[:]
+                )
+
+        by_k_rows = consts.tile([P, 256], BF16)
+        nc.vector.memset(by_k_rows[:], 0.0)
+        first_row = 0
+        for vec in (v2, v2_R, v1, u2, v1_R, u2_R):
+            rows = vec.shape[1] // 256
+            nc.scalar.dma_start(
+                out=by_k_rows[first_row : first_row + rows, :], in_=vec.rearrange("o (r c) -> (o r) c", c=256)
+            )
+            first_row += rows
+        by_o_rows = consts.tile([P, P], BF16)
+        nc.vector.memset(by_o_rows[:], 0.0)
+        o_tiles = OUT_F // P
+        for i, vec in enumerate((u1.rearrange("o f -> (o f)"), u1_R.rearrange("o f -> (o f)"), bias)):
+            nc.scalar.dma_start(
+                out=by_o_rows[o_tiles * i : o_tiles * (i + 1), :], in_=vec.rearrange("(r c) -> r c", c=P)
+            )
+
+        scratch = consts.tile([P, 1], F32)
+        nc.vector.memset(scratch[:], 0.0)
+        nc.scalar.activation(out=scratch[:], in_=scratch[:], func=ACT.Sign)
+
+        v_units = [open_v(0, 0)]
+        x_units = [open_x(0)]
+        v_units.append(open_v(0, 1))
+        x_units.append(open_x(1))
+        v_units.extend([open_v(1, 0), open_v(1, 1)])
+
+        sign_banks(v_units[0], ALL_BANKS)
+
+        by_k_bank = psum_v.tile([P, BANK], F32, tag="bank")
+        nc.tensor.transpose(by_k_bank[:, 0:P], by_k_rows[:].bitcast(F32), ident[:])
+        by_k = consts.tile([P, 2 * first_row], BF16)
+        nc.vector.tensor_copy(out=by_k[:], in_=by_k_bank[:].bitcast(BF16)[:, 0 : 2 * first_row])
+        v2_cols = (0, 16)
+        rank_scale = consts.tile([P, 2, 4], F32)
+        for path in range(2):
+            nc.vector.tensor_tensor(
+                out=rank_scale[:, path, :],
+                in0=by_k[:, 32 + 8 * path : 36 + 8 * path],
+                in1=by_k[:, 36 + 8 * path : 40 + 8 * path],
+                op=ALU.mult,
+            )
+        by_o_rows32 = consts.tile([P, P], F32)
+        nc.vector.tensor_copy(out=by_o_rows32[:], in_=by_o_rows[:])
+        by_o_bank = psum_v.tile([P, BANK], F32, tag="bank")
+        nc.tensor.transpose(by_o_bank[:, 0:P], by_o_rows32[:], ident[:])
+        by_o = consts.tile([P, 3 * o_tiles], F32)
+        nc.vector.tensor_copy(out=by_o[:], in_=by_o_bank[:, 0 : 3 * o_tiles])
+
+        x_banks(x_units[0], ALL_BANKS)
+        sign_banks(v_units[1], ALL_BANKS)
+        close_signs(v_units[0])
+        close_x(x_units[0])
+        x_banks(x_units[1], ALL_BANKS)
+        sign_banks(v_units[2], ALL_BANKS)
+        close_signs(v_units[1])
+        u_first = [open_u(0, 0), open_u(1, 0)]
+        sign_banks(v_units[3], ALL_BANKS)
+        close_signs(v_units[2])
+        close_x(x_units[1])
+        x_units.append(open_x(2))
+        u_second = [open_u(0, 1)]
+
+        waiting = v_units[3]
+        for path in range(2):
+            for j in range(2):
+                sign_banks(u_first[path], (2 * j, 2 * j + 1))
+                first_matmul((2 * j, 2 * j + 1), path)
+                if j == 0:
+                    close_signs(waiting)
+            close_h(path, 0)
+            waiting = u_first[path]
+        close_signs(waiting)
+        x_units.append(open_x(3))
+        u_second.append(open_u(1, 1))
+
+        y_t = second_matmul(0, 0)
+        x_banks(x_units[2], (0, 1))
+        late = (0, 0, y_t)
+        y_t = second_matmul(0, 1)
+        store(*late)
+        late = (0, 1, y_t)
+        x_banks(x_units[2], (2, 3))
+        close_x(x_units[2])
+
+        sign_banks(u_second[0], ALL_BANKS)
+        for path in range(2):
+            x_banks(x_units[3], (2 * path, 2 * path + 1))
+            sign_banks(u_second[1], (2 * path, 2 * path + 1))
+            first_matmul((4, 5), path)
+            close_signs(u_second[path])
+        close_x(x_units[3])
 
         for path in range(2):
-            for pair in range(2):
-                v_unit(path, pair)
-        x_unit(0)
-        x_unit(1)
-        first_matmul(0)
-        for path in range(2):
-            for part in range(2):
-                u_unit(path, part)
-        second_matmul(0)
-        x_unit(2)
-        x_unit(3)
-        first_matmul(1)
-        second_matmul(1)
+            y_t = second_matmul(0, 2 + path)
+            store(*late)
+            late = (0, 2 + path, y_t)
+            first_matmul((6, 7), path)
+            close_h(path, 1)
+
+        for o_group in range(OUT_F // BANK):
+            y_t = second_matmul(1, o_group)
+            store(*late)
+            late = (1, o_group, y_t)
+        store(*late)

@@ -173,10 +173,10 @@ def tile_littlebititqspeclinear_pa_kernel(
         def close_h(path, half):
             quantise(h_scaled[path], h_codes[path], h_scales[path], HALF * half, HALF)
 
-        def second_matmul(half, o_group):
+        def second_matmul(half, feature_tiles):
             tokens = slice(HALF * half, HALF * (half + 1))
             y_t = []
-            for a in range(4 * o_group, 4 * (o_group + 1)):
+            for a in feature_tiles:
                 features = slice(P * a, P * (a + 1))
                 sums = []
                 for path in range(2):
@@ -211,8 +211,8 @@ def tile_littlebititqspeclinear_pa_kernel(
                 y_t.append(both)
             return y_t
 
-        def store(half, o_group, y_t):
-            for i in range(HALF // P):
+        def store(half, o_group, y_t, token_tiles):
+            for i in token_tiles:
                 by_vector = half == 1 and i % 2 == 1
                 y_bank = (psum_v if by_vector else psum_s).tile([P, BANK], F32, tag="bank", name="y_bank")
                 for j in range(4):
@@ -226,6 +226,16 @@ def tile_littlebititqspeclinear_pa_kernel(
                 nc.sync.dma_start(
                     out=out2[first_token : first_token + P, BANK * o_group : BANK * (o_group + 1)], in_=y[:]
                 )
+
+        pending = {}
+
+        def feature_group(half, o_group):
+            y_t = []
+            for j in range(2):
+                y_t.extend(second_matmul(half, (4 * o_group + 2 * j, 4 * o_group + 2 * j + 1)))
+                if "group" in pending:
+                    store(*pending["group"], (2 * j, 2 * j + 1))
+            pending["group"] = (half, o_group, y_t)
 
         by_k_rows = consts.tile([P, 256], BF16)
         nc.vector.memset(by_k_rows[:], 0.0)
@@ -303,13 +313,9 @@ def tile_littlebititqspeclinear_pa_kernel(
         x_units.append(open_x(3))
         u_second.append(open_u(1, 1))
 
-        y_t = second_matmul(0, 0)
-        x_banks(x_units[2], (0, 1))
-        late = (0, 0, y_t)
-        y_t = second_matmul(0, 1)
-        store(*late)
-        late = (0, 1, y_t)
-        x_banks(x_units[2], (2, 3))
+        for o_group in range(2):
+            feature_group(0, o_group)
+            x_banks(x_units[2], (2 * o_group, 2 * o_group + 1))
         close_x(x_units[2])
 
         sign_banks(u_second[0], ALL_BANKS)
@@ -321,14 +327,10 @@ def tile_littlebititqspeclinear_pa_kernel(
         close_x(x_units[3])
 
         for path in range(2):
-            y_t = second_matmul(0, 2 + path)
-            store(*late)
-            late = (0, 2 + path, y_t)
+            feature_group(0, 2 + path)
             first_matmul((6, 7), path)
             close_h(path, 1)
 
         for o_group in range(OUT_F // BANK):
-            y_t = second_matmul(1, o_group)
-            store(*late)
-            late = (1, o_group, y_t)
-        store(*late)
+            feature_group(1, o_group)
+        store(*pending["group"], ALL_BANKS)

@@ -45,7 +45,6 @@ def tile_littlebititqspeclinear_pa_kernel(
         results = ctx.enter_context(tc.tile_pool(name="results", bufs=4))
         psum_s = ctx.enter_context(tc.psum_pool(name="psum_s", bufs=4))
         psum_v = ctx.enter_context(tc.psum_pool(name="psum_v", bufs=4))
-        ctx.enter_context(tc.manual_schedule())
 
         def mx_operand(name, columns):
             codes = [keep.tile([P, columns], U32, name="%s_codes%d" % (name, i), align_bytes=64) for i in range(2)]

@@ -198,7 +198,7 @@ def tile_littlebititqspeclinear_pa_kernel(
                     scale=by_o[:, a : a + 1],
                     bias=by_o[:, 2 * o_tiles + a : 2 * o_tiles + a + 1],
                 )
-                both = results.tile([P, HALF], F32, tag="both", bufs=8)
+                both = results.tile([P, HALF], F32, tag="both", bufs=6)
                 nc.vector.scalar_tensor_tensor(
                     out=both[:],
                     in0=sums[1][:],
@@ -210,46 +210,52 @@ def tile_littlebititqspeclinear_pa_kernel(
                 y_t.append(both)
             return y_t
 
-        def store(half, o_group, y_t, token_tiles):
-            for i in token_tiles:
-                by_vector = half == 1 and i % 2 == 1
+        def store(half, pair, y_t):
+            y = results.tile([P, HALF // P, 2 * P], F32, tag="y", bufs=3)
+            for j in range(2):
+                by_vector = half == 1 and j == 1
                 y_bank = (psum_v if by_vector else psum_s).tile([P, BANK], F32, tag="bank", name="y_bank")
-                for j in range(4):
-                    nc.tensor.transpose(y_bank[:, P * j : P * (j + 1)], y_t[j][:, P * i : P * (i + 1)], ident[:])
-                y = results.tile([P, BANK], F32, tag="y")
+                for i in range(HALF // P):
+                    nc.tensor.transpose(y_bank[:, P * i : P * (i + 1)], y_t[j][:, P * i : P * (i + 1)], ident[:])
+                by_tile = y_bank[:].rearrange("p (i f) -> p i f", f=P)
                 if by_vector:
-                    nc.vector.tensor_copy(out=y[:], in_=y_bank[:])
+                    nc.vector.tensor_copy(out=y[:, :, P * j : P * (j + 1)], in_=by_tile)
                 else:
-                    nc.scalar.copy(out=y[:], in_=y_bank[:])
-                first_token = HALF * half + P * i
-                nc.sync.dma_start(
-                    out=out2[first_token : first_token + P, BANK * o_group : BANK * (o_group + 1)], in_=y[:]
-                )
+                    nc.scalar.copy(out=y[:, :, P * j : P * (j + 1)], in_=by_tile)
+            nc.sync.dma_start(
+                out=out2[HALF * half : HALF * (half + 1), 2 * P * pair : 2 * P * (pair + 1)].rearrange(
+                    "(i p) f -> p i f", p=P
+                ),
+                in_=y[:],
+            )
 
         pending = {}
 
-        def feature_group(half, o_group):
-            y_t = []
-            for j in range(2):
-                y_t.extend(second_matmul(half, (4 * o_group + 2 * j, 4 * o_group + 2 * j + 1)))
-                if "group" in pending:
-                    store(*pending["group"], (2 * j, 2 * j + 1))
-            pending["group"] = (half, o_group, y_t)
+        def feature_pair(half, pair):
+            y_t = second_matmul(half, (2 * pair, 2 * pair + 1))
+            if "pair" in pending:
+                store(*pending["pair"])
+            pending["pair"] = (half, pair, y_t)
 
-        by_k_rows = consts.tile([P, 256], BF16)
-        nc.vector.memset(by_k_rows[:], 0.0)
-        first_row = 0
-        for vec in (v2, v2_R, v1, u2, v1_R, u2_R):
-            rows = vec.shape[1] // 256
-            nc.scalar.dma_start(
-                out=by_k_rows[first_row : first_row + rows, :], in_=vec.rearrange("o (r c) -> (o r) c", c=256)
-            )
-            first_row += rows
+        def rows_of_256(queue, vectors, name):
+            rows_tile = consts.tile([P, 256], BF16, name=name)
+            nc.vector.memset(rows_tile[:], 0.0)
+            first_row = 0
+            for vec in vectors:
+                rows = vec.shape[1] // 256
+                queue.dma_start(
+                    out=rows_tile[first_row : first_row + rows, :], in_=vec.rearrange("o (r c) -> (o r) c", c=256)
+                )
+                first_row += rows
+            return rows_tile
+
+        v2_rows = rows_of_256(nc.sync, (v2, v2_R), "v2_rows")
+        rank_rows = rows_of_256(nc.gpsimd, (v1, u2, v1_R, u2_R), "rank_rows")
         by_o_rows = consts.tile([P, P], BF16)
         nc.vector.memset(by_o_rows[:], 0.0)
         o_tiles = OUT_F // P
         for i, vec in enumerate((u1.rearrange("o f -> (o f)"), u1_R.rearrange("o f -> (o f)"), bias)):
-            nc.scalar.dma_start(
+            nc.gpsimd.dma_start(
                 out=by_o_rows[o_tiles * i : o_tiles * (i + 1), :], in_=vec.rearrange("(r c) -> r c", c=P)
             )
 
@@ -265,26 +271,15 @@ def tile_littlebititqspeclinear_pa_kernel(
 
         sign_banks(v_units[0], ALL_BANKS)
 
-        by_k_bank = psum_v.tile([P, BANK], F32, tag="bank")
-        nc.tensor.transpose(by_k_bank[:, 0:P], by_k_rows[:].bitcast(F32), ident[:])
-        by_k = consts.tile([P, 2 * first_row], BF16)
-        nc.vector.tensor_copy(out=by_k[:], in_=by_k_bank[:].bitcast(BF16)[:, 0 : 2 * first_row])
-        v2_cols = (0, 16)
-        rank_scale = consts.tile([P, 2, 4], F32)
-        for path in range(2):
-            nc.vector.tensor_tensor(
-                out=rank_scale[:, path, :],
-                in0=by_k[:, 32 + 8 * path : 36 + 8 * path],
-                in1=by_k[:, 36 + 8 * path : 40 + 8 * path],
-                op=ALU.mult,
-            )
-        by_o_rows32 = consts.tile([P, P], F32)
-        nc.vector.tensor_copy(out=by_o_rows32[:], in_=by_o_rows[:])
-        by_o_bank = psum_v.tile([P, BANK], F32, tag="bank")
-        nc.tensor.transpose(by_o_bank[:, 0:P], by_o_rows32[:], ident[:])
-        by_o = consts.tile([P, 3 * o_tiles], F32)
-        nc.vector.tensor_copy(out=by_o[:], in_=by_o_bank[:, 0 : 3 * o_tiles])
+        def onto_partitions(rows_tile, columns, name):
+            bank = psum_v.tile([P, BANK], F32, tag="bank", name=name + "_bank")
+            nc.tensor.transpose(bank[:, 0:P], rows_tile[:].bitcast(F32), ident[:])
+            table = consts.tile([P, columns], BF16, name=name)
+            nc.vector.tensor_copy(out=table[:], in_=bank[:].bitcast(BF16)[:, 0:columns])
+            return table
 
+        by_k = onto_partitions(v2_rows, 32, "by_k")
+        v2_cols = (0, 16)
         x_banks(x_units[0], ALL_BANKS)
         sign_banks(v_units[1], ALL_BANKS)
         close_signs(v_units[0])
@@ -299,6 +294,22 @@ def tile_littlebititqspeclinear_pa_kernel(
         x_units.append(open_x(2))
         u_second = [open_u(0, 1)]
 
+        by_rank = onto_partitions(rank_rows, 16, "by_rank")
+        rank_scale = consts.tile([P, 2, 4], F32)
+        for path in range(2):
+            nc.vector.tensor_tensor(
+                out=rank_scale[:, path, :],
+                in0=by_rank[:, 8 * path : 8 * path + 4],
+                in1=by_rank[:, 8 * path + 4 : 8 * path + 8],
+                op=ALU.mult,
+            )
+        by_o_rows32 = consts.tile([P, P], F32)
+        nc.vector.tensor_copy(out=by_o_rows32[:], in_=by_o_rows[:])
+        by_o_bank = psum_v.tile([P, BANK], F32, tag="bank")
+        nc.tensor.transpose(by_o_bank[:, 0:P], by_o_rows32[:], ident[:])
+        by_o = consts.tile([P, 3 * o_tiles], F32)
+        nc.vector.tensor_copy(out=by_o[:], in_=by_o_bank[:, 0 : 3 * o_tiles])
+
         waiting = v_units[3]
         for path in range(2):
             for j in range(2):
@@ -312,9 +323,9 @@ def tile_littlebititqspeclinear_pa_kernel(
         x_units.append(open_x(3))
         u_second.append(open_u(1, 1))
 
-        for o_group in range(2):
-            feature_group(0, o_group)
-            x_banks(x_units[2], (2 * o_group, 2 * o_group + 1))
+        for pair in range(4):
+            feature_pair(0, pair)
+            x_banks(x_units[2], (pair,))
         close_x(x_units[2])
 
         sign_banks(u_second[0], ALL_BANKS)
@@ -326,10 +337,11 @@ def tile_littlebititqspeclinear_pa_kernel(
         close_x(x_units[3])
 
         for path in range(2):
-            feature_group(0, 2 + path)
-            first_matmul((6, 7), path)
+            for j in range(2):
+                feature_pair(0, 4 + 2 * path + j)
+                first_matmul((6 + j,), path)
             close_h(path, 1)
 
-        for o_group in range(OUT_F // BANK):
-            feature_group(1, o_group)
-        store(*pending["group"], ALL_BANKS)
+        for pair in range(OUT_F // (2 * P)):
+            feature_pair(1, pair)
+        store(*pending["pair"])

@@ -22,7 +22,6 @@ IN_PASSES = IN_F // K_PASS
 UNIT = 4096
 UNIT_WORDS = UNIT // 4
 HALF = 512
-ALL_BANKS = (0, 1, 2, 3)
 
 FLOPS = 2 * (2 * TOKENS * IN_F * RANK + 2 * TOKENS * RANK * OUT_F)
 
@@ -40,7 +39,7 @@ def tile_littlebititqspeclinear_pa_kernel(
     with ExitStack() as ctx:
         consts = ctx.enter_context(tc.tile_pool(name="consts", bufs=1))
         keep = ctx.enter_context(tc.tile_pool(name="keep", bufs=1))
-        raws = ctx.enter_context(tc.tile_pool(name="raws", bufs=6))
+        raws = ctx.enter_context(tc.tile_pool(name="raws", bufs=10))
         groups = ctx.enter_context(tc.tile_pool(name="groups", bufs=1))
         results = ctx.enter_context(tc.tile_pool(name="results", bufs=4))
         psum_s = ctx.enter_context(tc.psum_pool(name="psum_s", bufs=4))
@@ -53,7 +52,8 @@ def tile_littlebititqspeclinear_pa_kernel(
 
         x_codes, x_scales = mx_operand("x", IN_PASSES * TOKENS)
         v_codes, v_scales = mx_operand("v", IN_PASSES * RANK)
-        u_codes, u_scales = mx_operand("u", OUT_F)
+        u_codes = keep.tile([P, 2 * OUT_F], U32, align_bytes=64)
+        u_scales = keep.tile([P, 2 * OUT_F], U8, align_bytes=64)
         h_codes, h_scales = mx_operand("h", TOKENS)
 
         def quantise(grouped, codes, scales, first, columns):
@@ -66,159 +66,197 @@ def tile_littlebititqspeclinear_pa_kernel(
         ident = consts.tile([P, P], F32)
         make_identity(nc, ident[:])
 
-        def load(rows, halve_columns):
-            raw = raws.tile([P, UNIT], BF16, tag="raw")
-            blocks, columns = rows.shape[1], rows.shape[2]
-            view = raw[:].rearrange("p (a c) -> p a c", a=blocks)
-            for half in range(2):
-                if halve_columns:
-                    part = slice(half * columns // 2, (half + 1) * columns // 2)
-                    nc.sync.dma_start(out=view[:, :, part], in_=rows[:, :, part])
-                else:
-                    part = slice(half * blocks // 2, (half + 1) * blocks // 2)
-                    nc.sync.dma_start(out=view[:, part, :], in_=rows[:, part, :])
-            return raw
+        def load_columns(rows, parts, which):
+            tiles = []
+            for i in which:
+                columns = IN_F // parts
+                raw = raws.tile([P, 2 * columns], BF16, name="raw%d" % parts, tag="raw%d" % parts, bufs=8 if parts == 4 else 10)
+                nc.sync.dma_start(
+                    out=raw[:].rearrange("p (s k) -> p s k", s=2), in_=rows[:, :, i * columns : (i + 1) * columns]
+                )
+                tiles.append(raw)
+            return tiles
 
         def transposed_bank(psum, unit, b):
-            words = unit["raw"][:].bitcast(F32)
+            per_tile = len(unit["raw"])
+            words = unit["raw"][b * per_tile // 4][:].bitcast(F32)
+            local = b % (4 // per_tile)
             bank = psum.tile([P, BANK], F32, tag="bank")
             for u in range(2):
                 for s in range(2):
-                    first = b * unit["bank_step"] + s * unit["block_step"] + P * u
+                    first = local * unit["bank_step"] + s * (unit["block_step"] // per_tile) + P * u
                     nc.tensor.transpose(
                         bank[:, 256 * u + P * s : 256 * u + P * (s + 1)], words[:, first : first + P], ident[:]
                     )
             return bank[:].bitcast(BF16).rearrange("p (u n e) -> p n u e", u=2, e=2)
 
-        def open_v(path, pair):
+        def open_v(path, pair, halves=(0, 1)):
             rows = (V, V_R)[path][256 * pair : 256 * (pair + 1), :].rearrange("(j s) k -> j s k", s=2)
             return {
-                "raw": load(rows, True), "bank_step": 256, "block_step": 1024,
+                "raw": load_columns(rows, 2, halves), "rows": rows, "bank_step": 256, "block_step": 1024,
                 "codes": v_codes[path], "scales": v_scales[path], "first": UNIT_WORDS * pair,
             }
 
-        def open_u(path, part):
-            rows = (U, U_R)[path][1024 * part : 1024 * (part + 1), :].rearrange("(a j) r -> j a r", j=P)
+        def open_u(group):
+            tiles = []
+            for matrix in (U, U_R):
+                raw = raws.tile([P, 2 * IN_F // 2], BF16, name="raw2", tag="raw2", bufs=10)
+                nc.sync.dma_start(
+                    out=raw[:].rearrange("p (a r) -> p a r", r=RANK),
+                    in_=matrix[512 * group : 512 * (group + 1), :].rearrange("(a j) r -> j a r", j=P),
+                )
+                tiles.append(raw)
             return {
-                "raw": load(rows, False), "bank_step": 512, "block_step": 256,
-                "codes": u_codes[path], "scales": u_scales[path], "first": UNIT_WORDS * part,
+                "raw": tiles, "bank_step": 512, "block_step": 512,
+                "codes": u_codes, "scales": u_scales, "first": UNIT_WORDS * group,
             }
 
-        def open_x(pair):
+        def open_x(pair, halves=(0, 1)):
             rows = x2[256 * pair : 256 * (pair + 1), :].rearrange("(s p) k -> p s k", p=P)
-            return {"raw": load(rows, True), "bank_step": 256, "block_step": 1024, "first": UNIT_WORDS * pair}
+            return {
+                "raw": load_columns(rows, 2, halves), "rows": rows, "bank_step": 256, "block_step": 1024,
+                "first": UNIT_WORDS * pair,
+            }
 
-        def sign_banks(unit, banks):
-            for b in banks:
+        banks, fetched, copied = {}, {"sign": 0, "x": 0}, {"sign": 0, "x": 0}
+
+        def fetch(stream, count=1):
+            for unit, b in streams[stream][fetched[stream] : fetched[stream] + count]:
+                psum = psum_s if stream == "sign" else psum_v
+                banks[(stream, fetched[stream])] = (unit, b, transposed_bank(psum, unit, b))
+                fetched[stream] += 1
+
+        def next_bank(stream):
+            if copied[stream] == fetched[stream]:
+                fetch(stream)
+            copied[stream] += 1
+            return banks[(stream, copied[stream] - 1)]
+
+        def sign_bank(count=1):
+            for i in range(count):
+                unit, b, values = next_bank("sign")
                 if b == 0:
-                    unit["signs"] = groups.tile([P, UNIT], BF16, name="signs", tag="signs", bufs=4, align_bytes=64)
-                values = transposed_bank(psum_s, unit, b)
+                    unit["signs"] = groups.tile([P, UNIT], BF16, name="signs", tag="signs", bufs=3, align_bytes=64)
                 nc.scalar.activation(out=as_words(unit["signs"], b), in_=values, func=ACT.Sign)
 
         def close_signs(unit):
             quantise(unit["signs"], unit["codes"], unit["scales"], unit["first"], UNIT_WORDS)
 
-        def x_banks(unit, banks):
-            for b in banks:
-                if b == 0:
-                    unit["scaled"] = [
-                        groups.tile([P, UNIT], BF16, name="scaled%d" % path, tag="scaled%d" % path, align_bytes=64)
-                        for path in range(2)
-                    ]
-                values = transposed_bank(psum_v, unit, b)
-                for path in range(2):
-                    v2_of_pass = by_k[:, v2_cols[path] + 4 * b : v2_cols[path] + 4 * (b + 1)]
-                    nc.vector.tensor_tensor(
-                        out=as_words(unit["scaled"][path], b),
-                        in0=values,
-                        in1=v2_of_pass.rearrange("p (u e) -> p u e", u=2).unsqueeze(1).to_broadcast([P, 256, 2, 2]),
-                        op=ALU.mult,
-                    )
-
-        def close_x(unit):
+        def x_bank():
+            unit, b, values = next_bank("x")
+            if b == 0:
+                unit["scaled"] = [
+                    groups.tile([P, UNIT], BF16, name="scaled%d" % path, tag="scaled%d" % path, align_bytes=64)
+                    for path in range(2)
+                ]
             for path in range(2):
+                v2_of_pass = by_k[:, v2_cols[path] + 4 * b : v2_cols[path] + 4 * (b + 1)]
+                nc.vector.tensor_tensor(
+                    out=as_words(unit["scaled"][path], b),
+                    in0=values,
+                    in1=v2_of_pass.rearrange("p (u e) -> p u e", u=2).unsqueeze(1).to_broadcast([P, 256, 2, 2]),
+                    op=ALU.mult,
+                )
+
+        def close_x(unit, paths=(0, 1)):
+            for path in paths:
                 quantise(unit["scaled"][path], x_codes[path], x_scales[path], unit["first"], UNIT_WORDS)
 
         h_scaled = [None, None]
 
-        def first_matmul(token_tiles, path):
-            for token_tile in token_tiles:
-                i = token_tile % (HALF // P)
-                if i == 0:
-                    h_scaled[path] = groups.tile(
-                        [P, 4 * HALF], BF16, name="h_scaled%d" % path, tag="h_scaled%d" % path, align_bytes=64
+        h_banks = {}
+
+        def first_matmul(token_tile, path):
+            tokens = UNIT_WORDS * (token_tile // 2) + P * (token_tile % 2)
+            h_bank = psum_v.tile([P, BANK], F32, tag="bank")
+            for t in range(4):
+                ranks = UNIT_WORDS * (t // 2) + P * (t % 2)
+                for c in range(IN_PASSES):
+                    nc.tensor.matmul_mx(
+                        out=h_bank[:, P * t : P * (t + 1)],
+                        lhsT=v_codes[path][:, ranks + 256 * c : ranks + 256 * c + P].bitcast(FP8X4),
+                        lhsT_scale=v_scales[path][:, ranks + 256 * c : ranks + 256 * c + P],
+                        rhs=x_codes[path][:, tokens + 256 * c : tokens + 256 * c + P].bitcast(FP8X4),
+                        rhs_scale=x_scales[path][:, tokens + 256 * c : tokens + 256 * c + P],
+                        start=(c == 0),
+                        stop=(c == IN_PASSES - 1),
                     )
-                tokens = UNIT_WORDS * (token_tile // 2) + P * (token_tile % 2)
-                h_bank = psum_v.tile([P, BANK], F32, tag="bank")
-                for t in range(4):
-                    ranks = UNIT_WORDS * (t // 2) + P * (t % 2)
-                    for c in range(IN_PASSES):
-                        nc.tensor.matmul_mx(
-                            out=h_bank[:, P * t : P * (t + 1)],
-                            lhsT=v_codes[path][:, ranks + 256 * c : ranks + 256 * c + P].bitcast(FP8X4),
-                            lhsT_scale=v_scales[path][:, ranks + 256 * c : ranks + 256 * c + P],
-                            rhs=x_codes[path][:, tokens + 256 * c : tokens + 256 * c + P].bitcast(FP8X4),
-                            rhs_scale=x_scales[path][:, tokens + 256 * c : tokens + 256 * c + P],
-                            start=(c == 0),
-                            stop=(c == IN_PASSES - 1),
-                        )
-                nc.vector.tensor_tensor(
-                    out=h_scaled[path][:, 4 * P * i : 4 * P * (i + 1)].rearrange("p (n t) -> p n t", t=4),
-                    in0=h_bank[:].rearrange("p (t n) -> p n t", t=4),
-                    in1=rank_scale[:, path, :].unsqueeze(1).to_broadcast([P, P, 4]),
-                    op=ALU.mult,
+            h_banks[(token_tile, path)] = h_bank
+
+        def scale_h(token_tile, path):
+            i = token_tile % (HALF // P)
+            if i == 0:
+                h_scaled[path] = groups.tile(
+                    [P, 4 * HALF], BF16, name="h_scaled%d" % path, tag="h_scaled%d" % path, align_bytes=64
                 )
+            nc.vector.tensor_tensor(
+                out=h_scaled[path][:, 4 * P * i : 4 * P * (i + 1)].rearrange("p (n t) -> p n t", t=4),
+                in0=h_banks[(token_tile, path)][:].rearrange("p (t n) -> p n t", t=4),
+                in1=rank_scale[:, path, :].unsqueeze(1).to_broadcast([P, P, 4]),
+                op=ALU.mult,
+            )
 
         def close_h(path, half):
             quantise(h_scaled[path], h_codes[path], h_scales[path], HALF * half, HALF)
 
-        def second_matmul(half, feature_tiles):
+        accs, primaries, sums, y_banks = {}, {}, {}, {}
+
+        def second_matmul(half, pair):
             tokens = slice(HALF * half, HALF * (half + 1))
-            y_t = []
-            for a in feature_tiles:
-                features = slice(P * a, P * (a + 1))
-                sums = []
+            for a in (2 * pair, 2 * pair + 1):
                 for path in range(2):
                     acc = (psum_s, psum_v)[path].tile([P, BANK], F32, tag="bank", name="acc%d" % path)
+                    first = UNIT_WORDS * (a // 4) + 4 * P * path + P * (a % 4)
                     nc.tensor.matmul_mx(
                         out=acc[:],
-                        lhsT=u_codes[path][:, features].bitcast(FP8X4),
-                        lhsT_scale=u_scales[path][:, features],
+                        lhsT=u_codes[:, first : first + P].bitcast(FP8X4),
+                        lhsT_scale=u_scales[:, first : first + P],
                         rhs=h_codes[path][:, tokens].bitcast(FP8X4),
                         rhs_scale=h_scales[path][:, tokens],
                         start=True,
                         stop=True,
                     )
-                    sums.append(acc)
+                    accs[(half, a, path)] = acc
+
+        def scale_primary(half, pair):
+            for a in (2 * pair, 2 * pair + 1):
                 primary = results.tile([P, HALF], F32, tag="primary")
                 nc.scalar.activation(
                     out=primary[:],
-                    in_=sums[0][:],
+                    in_=accs[(half, a, 0)][:],
                     func=ACT.Identity,
                     scale=by_o[:, a : a + 1],
                     bias=by_o[:, 2 * o_tiles + a : 2 * o_tiles + a + 1],
                 )
+                primaries[(half, a)] = primary
+
+        def add_residual(half, pair):
+            for a in (2 * pair, 2 * pair + 1):
                 both = results.tile([P, HALF], F32, tag="both", bufs=6)
                 nc.vector.scalar_tensor_tensor(
                     out=both[:],
-                    in0=sums[1][:],
+                    in0=accs[(half, a, 1)][:],
                     scalar=by_o[:, o_tiles + a : o_tiles + a + 1],
-                    in1=primary[:],
+                    in1=primaries[(half, a)][:],
                     op0=ALU.mult,
                     op1=ALU.add,
                 )
-                y_t.append(both)
-            return y_t
+                sums[(half, a)] = both
 
-        def store(half, pair, y_t):
+        def transpose_back(half, pair, split):
+            for j in range(2):
+                y_bank = (psum_v if split and j == 1 else psum_s).tile([P, BANK], F32, tag="bank", name="y_bank")
+                for i in range(HALF // P):
+                    nc.tensor.transpose(
+                        y_bank[:, P * i : P * (i + 1)], sums[(half, 2 * pair + j)][:, P * i : P * (i + 1)], ident[:]
+                    )
+                y_banks[(half, pair, j)] = y_bank
+
+        def store(half, pair, split):
             y = results.tile([P, HALF // P, 2 * P], F32, tag="y", bufs=3)
             for j in range(2):
-                by_vector = half == 1 and j == 1
-                y_bank = (psum_v if by_vector else psum_s).tile([P, BANK], F32, tag="bank", name="y_bank")
-                for i in range(HALF // P):
-                    nc.tensor.transpose(y_bank[:, P * i : P * (i + 1)], y_t[j][:, P * i : P * (i + 1)], ident[:])
-                by_tile = y_bank[:].rearrange("p (i f) -> p i f", f=P)
-                if by_vector:
+                by_tile = y_banks[(half, pair, j)][:].rearrange("p (i f) -> p i f", f=P)
+                if split and j == 1:
                     nc.vector.tensor_copy(out=y[:, :, P * j : P * (j + 1)], in_=by_tile)
                 else:
                     nc.scalar.copy(out=y[:, :, P * j : P * (j + 1)], in_=by_tile)
@@ -229,13 +267,9 @@ def tile_littlebititqspeclinear_pa_kernel(
                 in_=y[:],
             )
 
-        pending = {}
-
-        def feature_pair(half, pair):
-            y_t = second_matmul(half, (2 * pair, 2 * pair + 1))
-            if "pair" in pending:
-                store(*pending["pair"])
-            pending["pair"] = (half, pair, y_t)
+        scratch = consts.tile([P, 1], F32)
+        nc.vector.memset(scratch[:], 0.0)
+        nc.scalar.activation(out=scratch[:], in_=scratch[:], func=ACT.Sign)
 
         def rows_of_256(queue, vectors, name):
             rows_tile = consts.tile([P, 256], BF16, name=name)
@@ -250,51 +284,76 @@ def tile_littlebititqspeclinear_pa_kernel(
             return rows_tile
 
         v2_rows = rows_of_256(nc.sync, (v2, v2_R), "v2_rows")
-        rank_rows = rows_of_256(nc.gpsimd, (v1, u2, v1_R, u2_R), "rank_rows")
+        rank_rows = rows_of_256(nc.scalar, (v1, u2, v1_R, u2_R), "rank_rows")
         by_o_rows = consts.tile([P, P], BF16)
         nc.vector.memset(by_o_rows[:], 0.0)
         o_tiles = OUT_F // P
         for i, vec in enumerate((u1.rearrange("o f -> (o f)"), u1_R.rearrange("o f -> (o f)"), bias)):
-            nc.gpsimd.dma_start(
+            nc.scalar.dma_start(
                 out=by_o_rows[o_tiles * i : o_tiles * (i + 1), :], in_=vec.rearrange("(r c) -> r c", c=P)
             )
 
-        scratch = consts.tile([P, 1], F32)
-        nc.vector.memset(scratch[:], 0.0)
-        nc.scalar.activation(out=scratch[:], in_=scratch[:], func=ACT.Sign)
-
-        v_units = [open_v(0, 0)]
-        x_units = [open_x(0)]
+        ctx.enter_context(tc.manual_schedule())
+        x_units = [open_x(0, ())]
+        v_units = [open_v(0, 0, ())]
+        for i in range(4):
+            for unit in (x_units[0], v_units[0]):
+                unit["raw"].extend(load_columns(unit["rows"], 4, (i,)))
         v_units.append(open_v(0, 1))
         x_units.append(open_x(1))
         v_units.extend([open_v(1, 0), open_v(1, 1)])
-
-        sign_banks(v_units[0], ALL_BANKS)
-
-        def onto_partitions(rows_tile, columns, name):
-            bank = psum_v.tile([P, BANK], F32, tag="bank", name=name + "_bank")
-            nc.tensor.transpose(bank[:, 0:P], rows_tile[:].bitcast(F32), ident[:])
-            table = consts.tile([P, columns], BF16, name=name)
-            nc.vector.tensor_copy(out=table[:], in_=bank[:].bitcast(BF16)[:, 0:columns])
-            return table
-
-        by_k = onto_partitions(v2_rows, 32, "by_k")
-        v2_cols = (0, 16)
-        x_banks(x_units[0], ALL_BANKS)
-        sign_banks(v_units[1], ALL_BANKS)
-        close_signs(v_units[0])
-        close_x(x_units[0])
-        x_banks(x_units[1], ALL_BANKS)
-        sign_banks(v_units[2], ALL_BANKS)
-        close_signs(v_units[1])
-        u_first = [open_u(0, 0), open_u(1, 0)]
-        sign_banks(v_units[3], ALL_BANKS)
-        close_signs(v_units[2])
-        close_x(x_units[1])
+        u_units = [open_u(0)]
         x_units.append(open_x(2))
-        u_second = [open_u(0, 1)]
+        u_units.append(open_u(1))
+        x_units.append(open_x(3))
+        u_units.extend([open_u(2), open_u(3)])
+        streams = {
+            "sign": [(unit, b) for unit in v_units + u_units for b in range(4)],
+            "x": [(unit, b) for unit in x_units for b in range(4)],
+        }
 
-        by_rank = onto_partitions(rank_rows, 16, "by_rank")
+        def word_transpose(rows_tile, name):
+            bank = psum_v.tile([P, BANK], F32, tag="bank", name=name)
+            nc.tensor.transpose(bank[:, 0:P], rows_tile[:].bitcast(F32), ident[:])
+            return bank
+
+        def table(bank, columns, name):
+            values = consts.tile([P, columns], BF16, name=name)
+            nc.vector.tensor_copy(out=values[:], in_=bank[:].bitcast(BF16)[:, 0:columns])
+            return values
+
+        by_k = table(word_transpose(v2_rows, "by_k_bank"), 32, "by_k")
+        v2_cols = (0, 16)
+        for b in range(4):
+            x_bank()
+            sign_bank()
+        fetch("sign")
+        close_x(x_units[0], (0,))
+        sign_bank()
+        fetch("sign")
+        close_x(x_units[0], (1,))
+        sign_bank()
+
+        for i in range(2):
+            fetch("sign")
+            fetch("x", 1 + i)
+            x_bank()
+            sign_bank()
+        fetch("sign")
+        fetch("x")
+        x_bank()
+        sign_bank()
+        fetch("sign")
+        x_bank()
+        sign_bank()
+        for i in range(2):
+            fetch("sign")
+            close_signs(v_units[i])
+            sign_bank()
+        by_rank_bank = word_transpose(rank_rows, "by_rank_bank")
+        by_o_rows32 = consts.tile([P, P], F32)
+        nc.vector.tensor_copy(out=by_o_rows32[:], in_=by_o_rows[:])
+        by_rank = table(by_rank_bank, 16, "by_rank")
         rank_scale = consts.tile([P, 2, 4], F32)
         for path in range(2):
             nc.vector.tensor_tensor(
@@ -303,45 +362,99 @@ def tile_littlebititqspeclinear_pa_kernel(
                 in1=by_rank[:, 8 * path + 4 : 8 * path + 8],
                 op=ALU.mult,
             )
-        by_o_rows32 = consts.tile([P, P], F32)
-        nc.vector.tensor_copy(out=by_o_rows32[:], in_=by_o_rows[:])
+        for i in range(2):
+            fetch("sign")
+            first_matmul(i, 0)
+            close_x(x_units[1], (i,))
+            sign_bank()
         by_o_bank = psum_v.tile([P, BANK], F32, tag="bank")
         nc.tensor.transpose(by_o_bank[:, 0:P], by_o_rows32[:], ident[:])
         by_o = consts.tile([P, 3 * o_tiles], F32)
         nc.vector.tensor_copy(out=by_o[:], in_=by_o_bank[:, 0 : 3 * o_tiles])
+        fetch("x")
+        fetch("sign")
+        first_matmul(2, 0)
+        scale_h(0, 0)
+        scale_h(1, 0)
+        sign_bank()
+        fetch("sign")
+        first_matmul(3, 0)
+        close_signs(v_units[2])
+        sign_bank()
+        fetch("x")
+        fetch("sign")
+        x_bank()
+        sign_bank()
+        fetch("sign")
+        scale_h(2, 0)
+        scale_h(3, 0)
+        sign_bank()
+        fetch("sign", 2)
+        close_signs(v_units[3])
+        sign_bank()
+        first_matmul(0, 1)
+        fetch("sign")
+        first_matmul(1, 1)
+        close_h(0, 0)
+        x_bank()
+        sign_bank()
+        fetch("sign")
+        fetch("x")
+        first_matmul(2, 1)
+        scale_h(0, 1)
+        scale_h(1, 1)
+        sign_bank()
+        fetch("sign")
+        first_matmul(3, 1)
+        x_bank()
+        sign_bank()
+        fetch("x")
+        close_signs(u_units[0])
+        scale_h(2, 1)
+        scale_h(3, 1)
+        close_h(1, 0)
+        fetch("sign")
+        sign_bank()
+        x_bank()
+        sign_bank()
+        fetch("sign")
 
-        waiting = v_units[3]
-        for path in range(2):
-            for j in range(2):
-                sign_banks(u_first[path], (2 * j, 2 * j + 1))
-                first_matmul((2 * j, 2 * j + 1), path)
-                if j == 0:
-                    close_signs(waiting)
-            close_h(path, 0)
-            waiting = u_first[path]
-        close_signs(waiting)
-        x_units.append(open_x(3))
-        u_second.append(open_u(1, 1))
+        def step(pair, signs, xs, products, vector_work):
+            fetch("sign", signs)
+            fetch("x", xs)
+            for token_tile, path in products:
+                first_matmul(token_tile, path)
+            second_matmul(0, pair)
+            if pair > 0:
+                transpose_back(0, pair - 1, False)
+            sign_bank(signs)
+            scale_primary(0, pair)
+            for work in vector_work:
+                work()
+            add_residual(0, pair)
+            if pair > 0:
+                store(0, pair - 1, False)
 
-        for pair in range(4):
-            feature_pair(0, pair)
-            x_banks(x_units[2], (pair,))
-        close_x(x_units[2])
-
-        sign_banks(u_second[0], ALL_BANKS)
-        for path in range(2):
-            x_banks(x_units[3], (2 * path, 2 * path + 1))
-            sign_banks(u_second[1], (2 * path, 2 * path + 1))
-            first_matmul((4, 5), path)
-            close_signs(u_second[path])
-        close_x(x_units[3])
-
-        for path in range(2):
-            for j in range(2):
-                feature_pair(0, 4 + 2 * path + j)
-                first_matmul((6 + j,), path)
-            close_h(path, 1)
+        step(0, 2, 0, (), (lambda: close_x(x_units[2]),))
+        step(1, 2, 1, ((4, 0),), (x_bank, lambda: close_signs(u_units[1])))
+        step(2, 1, 1, ((5, 0),), (lambda: scale_h(4, 0), x_bank))
+        step(3, 1, 1, ((4, 1),), (x_bank, lambda: close_signs(u_units[2]), lambda: scale_h(5, 0)))
+        step(4, 1, 1, ((5, 1),), (lambda: scale_h(4, 1), x_bank))
+        step(5, 1, 0, (), (lambda: scale_h(5, 1), lambda: close_x(x_units[3]), lambda: close_signs(u_units[3])))
+        step(6, 0, 0, ((6, 0), (7, 0)), (lambda: scale_h(6, 0), lambda: scale_h(7, 0)))
+        step(7, 0, 0, ((6, 1), (7, 1)), (lambda: close_h(0, 1), lambda: scale_h(6, 1)))
+        scale_h(7, 1)
+        close_h(1, 1)
+        transpose_back(0, 7, True)
+        store(0, 7, True)
 
         for pair in range(OUT_F // (2 * P)):
-            feature_pair(1, pair)
-        store(*pending["pair"])
+            second_matmul(1, pair)
+            if pair > 0:
+                transpose_back(1, pair - 1, True)
+            scale_primary(1, pair)
+            add_residual(1, pair)
+            if pair > 0:
+                store(1, pair - 1, True)
+        transpose_back(1, 7, True)
+        store(1, 7, True)

@@ -252,20 +252,24 @@ def tile_littlebititqspeclinear_pa_kernel(
                     )
                 y_banks[(half, pair, j)] = y_bank
 
-        def store(half, pair, split):
-            y = results.tile([P, HALF // P, 2 * P], F32, tag="y", bufs=3)
-            for j in range(2):
-                by_tile = y_banks[(half, pair, j)][:].rearrange("p (i f) -> p i f", f=P)
-                if split and j == 1:
-                    nc.vector.tensor_copy(out=y[:, :, P * j : P * (j + 1)], in_=by_tile)
-                else:
-                    nc.scalar.copy(out=y[:, :, P * j : P * (j + 1)], in_=by_tile)
-            nc.sync.dma_start(
-                out=out2[HALF * half : HALF * (half + 1), 2 * P * pair : 2 * P * (pair + 1)].rearrange(
-                    "(i p) f -> p i f", p=P
-                ),
-                in_=y[:],
-            )
+        def store(half, pair, split, parts=1):
+            tiles = HALF // P // parts
+            for part in range(parts):
+                y = results.tile([P, tiles, 2 * P], F32, tag="y", bufs=3)
+                for j in range(2):
+                    y_bank = y_banks[(half, pair, j)][:, P * tiles * part : P * tiles * (part + 1)]
+                    by_tile = y_bank.rearrange("p (i f) -> p i f", f=P)
+                    if split and j == 1:
+                        nc.vector.tensor_copy(out=y[:, :, P * j : P * (j + 1)], in_=by_tile)
+                    else:
+                        nc.scalar.copy(out=y[:, :, P * j : P * (j + 1)], in_=by_tile)
+                first = HALF * half + P * tiles * part
+                nc.sync.dma_start(
+                    out=out2[first : first + P * tiles, 2 * P * pair : 2 * P * (pair + 1)].rearrange(
+                        "(i p) f -> p i f", p=P
+                    ),
+                    in_=y[:],
+                )
 
         scratch = consts.tile([P, 1], F32)
         nc.vector.memset(scratch[:], 0.0)
@@ -362,11 +366,14 @@ def tile_littlebititqspeclinear_pa_kernel(
                 in1=by_rank[:, 8 * path + 4 : 8 * path + 8],
                 op=ALU.mult,
             )
-        for i in range(2):
-            fetch("sign")
-            first_matmul(i, 0)
-            close_x(x_units[1], (i,))
-            sign_bank()
+        fetch("sign", 2)
+        first_matmul(0, 0)
+        first_matmul(1, 0)
+        close_x(x_units[1], (0,))
+        sign_bank()
+        fetch("sign")
+        close_x(x_units[1], (1,))
+        sign_bank()
         by_o_bank = psum_v.tile([P, BANK], F32, tag="bank")
         nc.tensor.transpose(by_o_bank[:, 0:P], by_o_rows32[:], ident[:])
         by_o = consts.tile([P, 3 * o_tiles], F32)
@@ -374,46 +381,45 @@ def tile_littlebititqspeclinear_pa_kernel(
         fetch("x")
         fetch("sign")
         first_matmul(2, 0)
+        first_matmul(3, 0)
         scale_h(0, 0)
         scale_h(1, 0)
         sign_bank()
-        fetch("sign")
-        first_matmul(3, 0)
         close_signs(v_units[2])
         sign_bank()
         fetch("x")
-        fetch("sign")
+        fetch("sign", 2)
         x_bank()
         sign_bank()
         fetch("sign")
         scale_h(2, 0)
         scale_h(3, 0)
         sign_bank()
-        fetch("sign", 2)
+        fetch("sign")
         close_signs(v_units[3])
         sign_bank()
-        first_matmul(0, 1)
+        fetch("x")
         fetch("sign")
+        first_matmul(0, 1)
         first_matmul(1, 1)
         close_h(0, 0)
         x_bank()
         sign_bank()
         fetch("sign")
-        fetch("x")
-        first_matmul(2, 1)
         scale_h(0, 1)
         scale_h(1, 1)
         sign_bank()
         fetch("sign")
+        first_matmul(2, 1)
         first_matmul(3, 1)
         x_bank()
         sign_bank()
         fetch("x")
+        fetch("sign")
         close_signs(u_units[0])
         scale_h(2, 1)
         scale_h(3, 1)
         close_h(1, 0)
-        fetch("sign")
         sign_bank()
         x_bank()
         sign_bank()
@@ -436,13 +442,13 @@ def tile_littlebititqspeclinear_pa_kernel(
                 store(0, pair - 1, False)
 
         step(0, 2, 0, (), (lambda: close_x(x_units[2]),))
-        step(1, 2, 1, ((4, 0),), (x_bank, lambda: close_signs(u_units[1])))
+        step(1, 2, 2, ((4, 0),), (x_bank, lambda: close_signs(u_units[1]), x_bank))
         step(2, 1, 1, ((5, 0),), (lambda: scale_h(4, 0), x_bank))
-        step(3, 1, 1, ((4, 1),), (x_bank, lambda: close_signs(u_units[2]), lambda: scale_h(5, 0)))
-        step(4, 1, 1, ((5, 1),), (lambda: scale_h(4, 1), x_bank))
-        step(5, 1, 0, (), (lambda: scale_h(5, 1), lambda: close_x(x_units[3]), lambda: close_signs(u_units[3])))
-        step(6, 0, 0, ((6, 0), (7, 0)), (lambda: scale_h(6, 0), lambda: scale_h(7, 0)))
-        step(7, 0, 0, ((6, 1), (7, 1)), (lambda: close_h(0, 1), lambda: scale_h(6, 1)))
+        step(3, 1, 1, ((4, 1),), (lambda: close_signs(u_units[2]), lambda: scale_h(5, 0), x_bank))
+        step(4, 1, 0, ((5, 1),), (lambda: close_x(x_units[3], (0,)), lambda: scale_h(4, 1), lambda: close_x(x_units[3], (1,))))
+        step(5, 1, 0, ((6, 0),), (lambda: scale_h(5, 1), lambda: close_signs(u_units[3])))
+        step(6, 0, 0, ((7, 0),), (lambda: scale_h(6, 0),))
+        step(7, 0, 0, ((6, 1), (7, 1)), (lambda: scale_h(7, 0), lambda: close_h(0, 1), lambda: scale_h(6, 1)))
         scale_h(7, 1)
         close_h(1, 1)
         transpose_back(0, 7, True)
@@ -457,4 +463,4 @@ def tile_littlebititqspeclinear_pa_kernel(
             if pair > 0:
                 store(1, pair - 1, True)
         transpose_back(1, 7, True)
-        store(1, 7, True)
+        store(1, 7, True, 2)

@@ -200,6 +200,7 @@ def tile_littlebititqspeclinear_pa_kernel(
             quantise(h_scaled[path], h_codes[path], h_scales[path], HALF * half, HALF)
 
         accs, primaries, sums, y_banks = {}, {}, {}, {}
+        added_in_psum = [(0, 1), (0, 15)]
 
         def second_matmul(half, pair):
             tokens = slice(HALF * half, HALF * (half + 1))
@@ -229,9 +230,17 @@ def tile_littlebititqspeclinear_pa_kernel(
                     bias=by_o[:, 2 * o_tiles + a : 2 * o_tiles + a + 1],
                 )
                 primaries[(half, a)] = primary
+                if (half, a) in added_in_psum:
+                    residual = results.tile([P, HALF], F32, tag="residual", bufs=2)
+                    nc.scalar.activation(
+                        out=residual[:], in_=accs[(half, a, 1)][:], func=ACT.Copy, scale=by_o[:, o_tiles + a : o_tiles + a + 1]
+                    )
+                    sums[(half, a)] = residual
 
         def add_residual(half, pair):
             for a in (2 * pair, 2 * pair + 1):
+                if (half, a) in added_in_psum:
+                    continue
                 both = results.tile([P, HALF], F32, tag="both", bufs=6)
                 nc.vector.scalar_tensor_tensor(
                     out=both[:],
@@ -246,10 +255,18 @@ def tile_littlebititqspeclinear_pa_kernel(
         def transpose_back(half, pair, split):
             for j in range(2):
                 y_bank = (psum_v if split and j == 1 else psum_s).tile([P, BANK], F32, tag="bank", name="y_bank")
+                a = 2 * pair + j
+                parts = (primaries[(half, a)], sums[(half, a)]) if (half, a) in added_in_psum else (sums[(half, a)],)
                 for i in range(HALF // P):
-                    nc.tensor.transpose(
-                        y_bank[:, P * i : P * (i + 1)], sums[(half, 2 * pair + j)][:, P * i : P * (i + 1)], ident[:]
-                    )
+                    for n, part in enumerate(parts):
+                        nc.tensor.matmul(
+                            y_bank[:, P * i : P * (i + 1)],
+                            lhsT=part[:, P * i : P * (i + 1)],
+                            rhs=ident[:],
+                            is_transpose=True,
+                            start=(n == 0),
+                            stop=(n == len(parts) - 1),
+                        )
                 y_banks[(half, pair, j)] = y_bank
 
         def store(half, pair, split, parts=1):

@@ -343,6 +343,7 @@ def tile_littlebititqspeclinear_pa_kernel(
             nc.vector.tensor_copy(out=values[:], in_=bank[:].bitcast(BF16)[:, 0:columns])
             return values
 
+        fetch("x")
         by_k = table(word_transpose(v2_rows, "by_k_bank"), 32, "by_k")
         v2_cols = (0, 16)
         for b in range(4):
@@ -442,12 +443,15 @@ def tile_littlebititqspeclinear_pa_kernel(
         sign_bank()
         fetch("sign")
 
-        def step(pair, signs, xs, products, vector_work):
-            fetch("sign", signs)
+        def step(pair, signs, xs, products, vector_work, vector_work_after=()):
             fetch("x", xs)
+            fetch("sign", signs)
+            if pair == 7:
+                second_matmul(0, pair)
             for token_tile, path in products:
                 first_matmul(token_tile, path)
-            second_matmul(0, pair)
+            if pair < 7:
+                second_matmul(0, pair)
             if pair > 0:
                 transpose_back(0, pair - 1, False)
             sign_bank(signs)
@@ -455,11 +459,13 @@ def tile_littlebititqspeclinear_pa_kernel(
             for work in vector_work:
                 work()
             add_residual(0, pair)
+            for work in vector_work_after:
+                work()
             if pair > 0:
                 store(0, pair - 1, False)
 
         step(0, 2, 0, (), (lambda: close_x(x_units[2]),))
-        step(1, 2, 2, ((4, 0),), (x_bank, lambda: close_signs(u_units[1]), x_bank))
+        step(1, 2, 2, ((4, 0),), (x_bank, lambda: close_signs(u_units[1])), (x_bank,))
         step(2, 1, 1, ((5, 0),), (lambda: scale_h(4, 0), x_bank))
         step(3, 1, 1, ((4, 1),), (lambda: close_signs(u_units[2]), lambda: scale_h(5, 0), x_bank))
         step(4, 1, 0, ((5, 1),), (lambda: close_x(x_units[3], (0,)), lambda: scale_h(4, 1), lambda: close_x(x_units[3], (1,))))

@@ -65,6 +65,8 @@ def tile_littlebititqspeclinear_pa_kernel(
 
         ident = consts.tile([P, P], F32)
         make_identity(nc, ident[:])
+        ident_bf16 = consts.tile([P, P], BF16)
+        make_identity(nc, ident_bf16[:])
 
         def load_columns(rows, parts, which):
             tiles = []
@@ -200,7 +202,7 @@ def tile_littlebititqspeclinear_pa_kernel(
             quantise(h_scaled[path], h_codes[path], h_scales[path], HALF * half, HALF)
 
         accs, primaries, sums, y_banks = {}, {}, {}, {}
-        added_in_psum = [(0, 1), (0, 15)]
+        added_in_psum = [(0, 1), (0, 3), (0, 15)]
 
         def second_matmul(half, pair):
             tokens = slice(HALF * half, HALF * (half + 1))
@@ -272,7 +274,7 @@ def tile_littlebititqspeclinear_pa_kernel(
         def store(half, pair, split, parts=1):
             tiles = HALF // P // parts
             for part in range(parts):
-                y = results.tile([P, tiles, 2 * P], F32, tag="y", bufs=3)
+                y = results.tile([P, tiles, 2 * P], F32, tag="y", bufs=4)
                 for j in range(2):
                     y_bank = y_banks[(half, pair, j)][:, P * tiles * part : P * tiles * (part + 1)]
                     by_tile = y_bank.rearrange("p (i f) -> p i f", f=P)
@@ -373,17 +375,10 @@ def tile_littlebititqspeclinear_pa_kernel(
             close_signs(v_units[i])
             sign_bank()
         by_rank_bank = word_transpose(rank_rows, "by_rank_bank")
-        by_o_rows32 = consts.tile([P, P], F32)
-        nc.vector.tensor_copy(out=by_o_rows32[:], in_=by_o_rows[:])
         by_rank = table(by_rank_bank, 16, "by_rank")
         rank_scale = consts.tile([P, 2, 4], F32)
-        for path in range(2):
-            nc.vector.tensor_tensor(
-                out=rank_scale[:, path, :],
-                in0=by_rank[:, 8 * path : 8 * path + 4],
-                in1=by_rank[:, 8 * path + 4 : 8 * path + 8],
-                op=ALU.mult,
-            )
+        by_path = by_rank[:].rearrange("p (q w t) -> p q w t", q=2, w=2)
+        nc.gpsimd.tensor_tensor(out=rank_scale[:], in0=by_path[:, :, 0, :], in1=by_path[:, :, 1, :], op=ALU.mult)
         fetch("sign", 2)
         first_matmul(0, 0)
         first_matmul(1, 0)
@@ -393,9 +388,9 @@ def tile_littlebititqspeclinear_pa_kernel(
         close_x(x_units[1], (1,))
         sign_bank()
         by_o_bank = psum_v.tile([P, BANK], F32, tag="bank")
-        nc.tensor.transpose(by_o_bank[:, 0:P], by_o_rows32[:], ident[:])
+        nc.tensor.transpose(by_o_bank[:].bitcast(BF16)[:, 0:P], by_o_rows[:], ident_bf16[:])
         by_o = consts.tile([P, 3 * o_tiles], F32)
-        nc.vector.tensor_copy(out=by_o[:], in_=by_o_bank[:, 0 : 3 * o_tiles])
+        nc.scalar.copy(out=by_o[:], in_=by_o_bank[:].bitcast(BF16)[:, 0 : 3 * o_tiles])
         fetch("x")
         fetch("sign")
         first_matmul(2, 0)
@@ -432,8 +427,8 @@ def tile_littlebititqspeclinear_pa_kernel(
         first_matmul(3, 1)
         x_bank()
         sign_bank()
-        fetch("x")
         fetch("sign")
+        fetch("x")
         close_signs(u_units[0])
         scale_h(2, 1)
         scale_h(3, 1)
@@ -464,14 +459,17 @@ def tile_littlebititqspeclinear_pa_kernel(
             if pair > 0:
                 store(0, pair - 1, False)
 
-        step(0, 2, 0, (), (lambda: close_x(x_units[2]),))
-        step(1, 2, 2, ((4, 0),), (x_bank, lambda: close_signs(u_units[1])), (x_bank,))
-        step(2, 1, 1, ((5, 0),), (lambda: scale_h(4, 0), x_bank))
-        step(3, 1, 1, ((4, 1),), (lambda: close_signs(u_units[2]), lambda: scale_h(5, 0), x_bank))
-        step(4, 1, 0, ((5, 1),), (lambda: close_x(x_units[3], (0,)), lambda: scale_h(4, 1), lambda: close_x(x_units[3], (1,))))
-        step(5, 1, 0, ((6, 0),), (lambda: scale_h(5, 1), lambda: close_signs(u_units[3])))
-        step(6, 0, 0, ((7, 0),), (lambda: scale_h(6, 0),))
-        step(7, 0, 0, ((6, 1), (7, 1)), (lambda: scale_h(7, 0), lambda: close_h(0, 1), lambda: scale_h(6, 1)))
+        step(0, 1, 0, (), (lambda: close_x(x_units[2]),))
+        step(1, 3, 1, ((4, 0), (4, 1)), (x_bank, lambda: close_signs(u_units[1])), (lambda: scale_h(4, 0), lambda: scale_h(4, 1)))
+        step(2, 2, 3, ((5, 0),), (x_bank, x_bank, x_bank), (lambda: scale_h(5, 0),))
+        step(
+            3, 1, 0, ((5, 1),),
+            (lambda: close_x(x_units[3], (0,)), lambda: close_signs(u_units[2])), (lambda: scale_h(5, 1),),
+        )
+        step(4, 0, 0, ((6, 0),), (lambda: scale_h(6, 0),), (lambda: close_x(x_units[3], (1,)),))
+        step(5, 1, 0, ((7, 0),), (lambda: close_signs(u_units[3]),))
+        step(6, 0, 0, ((6, 1),), (lambda: scale_h(7, 0),))
+        step(7, 0, 0, ((7, 1),), (lambda: close_h(0, 1), lambda: scale_h(6, 1)))
         scale_h(7, 1)
         close_h(1, 1)
         transpose_back(0, 7, True)

@@ -63,6 +63,20 @@ def tile_littlebititqspeclinear_pa_kernel(
                 in_=grouped[:],
             )
 
+        def rows_of_256(queue, zeroing, vectors, name):
+            rows_tile = consts.tile([P, 256], BF16, name=name)
+            zeroing.memset(rows_tile[:], 0.0)
+            first_row = 0
+            for vec in vectors:
+                rows = vec.shape[1] // 256
+                queue.dma_start(
+                    out=rows_tile[first_row : first_row + rows, :], in_=vec.rearrange("o (r c) -> (o r) c", c=256)
+                )
+                first_row += rows
+            return rows_tile
+
+        v2_rows = rows_of_256(nc.sync, nc.gpsimd, (v2, v2_R), "v2_rows")
+
         ident = consts.tile([P, P], F32)
         make_identity(nc, ident[:])
         ident_bf16 = consts.tile([P, P], BF16)
@@ -243,7 +257,7 @@ def tile_littlebititqspeclinear_pa_kernel(
             for a in (2 * pair, 2 * pair + 1):
                 if (half, a) in added_in_psum:
                     continue
-                both = results.tile([P, HALF], F32, tag="both", bufs=6)
+                both = results.tile([P, HALF], F32, tag="both", bufs=5)
                 nc.vector.scalar_tensor_tensor(
                     out=both[:],
                     in0=accs[(half, a, 1)][:],
@@ -254,30 +268,36 @@ def tile_littlebititqspeclinear_pa_kernel(
                 )
                 sums[(half, a)] = both
 
-        def transpose_back(half, pair, split):
+        def transpose_back(half, pair, split, parts=1):
+            tiles = HALF // P // parts
             for j in range(2):
-                y_bank = (psum_v if split and j == 1 else psum_s).tile([P, BANK], F32, tag="bank", name="y_bank")
+                y_banks[(half, pair, j)] = []
                 a = 2 * pair + j
-                parts = (primaries[(half, a)], sums[(half, a)]) if (half, a) in added_in_psum else (sums[(half, a)],)
+                terms = (primaries[(half, a)], sums[(half, a)]) if (half, a) in added_in_psum else (sums[(half, a)],)
                 for i in range(HALF // P):
-                    for n, part in enumerate(parts):
+                    if i % tiles == 0:
+                        y_bank = (psum_v if split and j == 1 else psum_s).tile([P, BANK], F32, tag="bank", name="y_bank")
+                        y_banks[(half, pair, j)].append(y_bank)
+                    for n, term in enumerate(terms):
                         nc.tensor.matmul(
-                            y_bank[:, P * i : P * (i + 1)],
-                            lhsT=part[:, P * i : P * (i + 1)],
+                            y_bank[:, P * (i % tiles) : P * (i % tiles + 1)],
+                            lhsT=term[:, P * i : P * (i + 1)],
                             rhs=ident[:],
                             is_transpose=True,
                             start=(n == 0),
-                            stop=(n == len(parts) - 1),
+                            stop=(n == len(terms) - 1),
                         )
-                y_banks[(half, pair, j)] = y_bank
 
         def store(half, pair, split, parts=1):
             tiles = HALF // P // parts
             for part in range(parts):
-                y = results.tile([P, tiles, 2 * P], F32, tag="y", bufs=4)
+                y = results.tile(
+                    [P, tiles, 2 * P], F32, name="y", tag="y" if parts == 1 else "y_part", bufs=3 if parts == 1 else 4
+                )
                 for j in range(2):
-                    y_bank = y_banks[(half, pair, j)][:, P * tiles * part : P * tiles * (part + 1)]
-                    by_tile = y_bank.rearrange("p (i f) -> p i f", f=P)
+                    banks = y_banks[(half, pair, j)]
+                    bank, offset = divmod(HALF * part // parts, HALF // len(banks))
+                    by_tile = banks[bank][:, offset : offset + P * tiles].rearrange("p (i f) -> p i f", f=P)
                     if split and j == 1:
                         nc.vector.tensor_copy(out=y[:, :, P * j : P * (j + 1)], in_=by_tile)
                     else:
@@ -294,20 +314,7 @@ def tile_littlebititqspeclinear_pa_kernel(
         nc.vector.memset(scratch[:], 0.0)
         nc.scalar.activation(out=scratch[:], in_=scratch[:], func=ACT.Sign)
 
-        def rows_of_256(queue, vectors, name):
-            rows_tile = consts.tile([P, 256], BF16, name=name)
-            nc.vector.memset(rows_tile[:], 0.0)
-            first_row = 0
-            for vec in vectors:
-                rows = vec.shape[1] // 256
-                queue.dma_start(
-                    out=rows_tile[first_row : first_row + rows, :], in_=vec.rearrange("o (r c) -> (o r) c", c=256)
-                )
-                first_row += rows
-            return rows_tile
-
-        v2_rows = rows_of_256(nc.sync, (v2, v2_R), "v2_rows")
-        rank_rows = rows_of_256(nc.scalar, (v1, u2, v1_R, u2_R), "rank_rows")
+        rank_rows = rows_of_256(nc.scalar, nc.vector, (v1, u2, v1_R, u2_R), "rank_rows")
         by_o_rows = consts.tile([P, P], BF16)
         nc.vector.memset(by_o_rows[:], 0.0)
         o_tiles = OUT_F // P
@@ -340,13 +347,13 @@ def tile_littlebititqspeclinear_pa_kernel(
             nc.tensor.transpose(bank[:, 0:P], rows_tile[:].bitcast(F32), ident[:])
             return bank
 
-        def table(bank, columns, name):
+        def table(copy, bank, columns, name):
             values = consts.tile([P, columns], BF16, name=name)
-            nc.vector.tensor_copy(out=values[:], in_=bank[:].bitcast(BF16)[:, 0:columns])
+            copy(out=values[:], in_=bank[:].bitcast(BF16)[:, 0:columns])
             return values
 
+        by_k = table(nc.vector.tensor_copy, word_transpose(v2_rows, "by_k_bank"), 32, "by_k")
         fetch("x")
-        by_k = table(word_transpose(v2_rows, "by_k_bank"), 32, "by_k")
         v2_cols = (0, 16)
         for b in range(4):
             x_bank()
@@ -375,7 +382,7 @@ def tile_littlebititqspeclinear_pa_kernel(
             close_signs(v_units[i])
             sign_bank()
         by_rank_bank = word_transpose(rank_rows, "by_rank_bank")
-        by_rank = table(by_rank_bank, 16, "by_rank")
+        by_rank = table(nc.scalar.copy, by_rank_bank, 16, "by_rank")
         rank_scale = consts.tile([P, 2, 4], F32)
         by_path = by_rank[:].rearrange("p (q w t) -> p q w t", q=2, w=2)
         nc.gpsimd.tensor_tensor(out=rank_scale[:], in0=by_path[:, :, 0, :], in1=by_path[:, :, 1, :], op=ALU.mult)
@@ -478,10 +485,10 @@ def tile_littlebititqspeclinear_pa_kernel(
         for pair in range(OUT_F // (2 * P)):
             second_matmul(1, pair)
             if pair > 0:
-                transpose_back(1, pair - 1, True)
+                transpose_back(1, pair - 1, pair < 7)
             scale_primary(1, pair)
             add_residual(1, pair)
             if pair > 0:
-                store(1, pair - 1, True)
-        transpose_back(1, 7, True)
+                store(1, pair - 1, pair < 7, 1 if pair < 7 else 2)
+        transpose_back(1, 7, True, 2)
         store(1, 7, True, 2)

@@ -291,9 +291,10 @@ def tile_littlebititqspeclinear_pa_kernel(
         def store(half, pair, split, parts=1):
             tiles = HALF // P // parts
             for part in range(parts):
-                y = results.tile(
-                    [P, tiles, 2 * P], F32, name="y", tag="y" if parts == 1 else "y_part", bufs=3 if parts == 1 else 4
-                )
+                if parts == 1:
+                    y = raws.tile([P, tiles, 2 * P], F32, name="y", tag="raw2", bufs=10)
+                else:
+                    y = results.tile([P, tiles, 2 * P], F32, name="y_part", tag="y_part", bufs=4)
                 for j in range(2):
                     banks = y_banks[(half, pair, j)]
                     bank, offset = divmod(HALF * part // parts, HALF // len(banks))

@@ -483,13 +483,15 @@ def tile_littlebititqspeclinear_pa_kernel(
         transpose_back(0, 7, True)
         store(0, 7, True)
 
-        for pair in range(OUT_F // (2 * P)):
-            second_matmul(1, pair)
-            if pair > 0:
-                transpose_back(1, pair - 1, pair < 7)
-            scale_primary(1, pair)
-            add_residual(1, pair)
-            if pair > 0:
-                store(1, pair - 1, pair < 7, 1 if pair < 7 else 2)
+        for made, back in (((0, 1, 2), (0, 1)), ((3, 4), (2, 3)), ((5,), (4,)), ((6,), (5,)), ((7,), (6,))):
+            for pair in made:
+                second_matmul(1, pair)
+            for pair in made:
+                scale_primary(1, pair)
+                add_residual(1, pair)
+            for pair in back:
+                transpose_back(1, pair, pair < 6)
+            for pair in back:
+                store(1, pair, pair < 6, 1 if pair < 6 else 2)
         transpose_back(1, 7, True, 2)
         store(1, 7, True, 2)

@@ -364,6 +364,7 @@ def tile_littlebititqspeclinear_pa_kernel(
         sign_bank()
         fetch("sign")
         close_x(x_units[0], (1,))
+        close_signs(v_units[0])
         sign_bank()
 
         for i in range(2):
@@ -373,22 +374,22 @@ def tile_littlebititqspeclinear_pa_kernel(
             sign_bank()
         fetch("sign")
         fetch("x")
-        x_bank()
         sign_bank()
         fetch("sign")
+        close_signs(v_units[1])
         x_bank()
         sign_bank()
+        x_bank()
         for i in range(2):
             fetch("sign")
-            close_signs(v_units[i])
             sign_bank()
         by_rank_bank = word_transpose(rank_rows, "by_rank_bank")
         by_rank = table(nc.scalar.copy, by_rank_bank, 16, "by_rank")
         rank_scale = consts.tile([P, 2, 4], F32)
         by_path = by_rank[:].rearrange("p (q w t) -> p q w t", q=2, w=2)
         nc.gpsimd.tensor_tensor(out=rank_scale[:], in0=by_path[:, :, 0, :], in1=by_path[:, :, 1, :], op=ALU.mult)
-        fetch("sign", 2)
         first_matmul(0, 0)
+        fetch("sign", 2)
         first_matmul(1, 0)
         close_x(x_units[1], (0,))
         sign_bank()
@@ -399,7 +400,6 @@ def tile_littlebititqspeclinear_pa_kernel(
         nc.tensor.transpose(by_o_bank[:].bitcast(BF16)[:, 0:P], by_o_rows[:], ident_bf16[:])
         by_o = consts.tile([P, 3 * o_tiles], F32)
         nc.scalar.copy(out=by_o[:], in_=by_o_bank[:].bitcast(BF16)[:, 0 : 3 * o_tiles])
-        fetch("x")
         fetch("sign")
         first_matmul(2, 0)
         first_matmul(3, 0)
@@ -408,9 +408,9 @@ def tile_littlebititqspeclinear_pa_kernel(
         sign_bank()
         close_signs(v_units[2])
         sign_bank()
-        fetch("x")
-        fetch("sign", 2)
-        x_bank()
+        fetch("sign")
+        fetch("x", 2)
+        fetch("sign")
         sign_bank()
         fetch("sign")
         scale_h(2, 0)
@@ -418,6 +418,7 @@ def tile_littlebititqspeclinear_pa_kernel(
         sign_bank()
         fetch("sign")
         close_signs(v_units[3])
+        x_bank()
         sign_bank()
         fetch("x")
         fetch("sign")
@@ -447,8 +448,9 @@ def tile_littlebititqspeclinear_pa_kernel(
         fetch("sign")
 
         def step(pair, signs, xs, products, vector_work, vector_work_after=()):
+            fetch("sign", min(signs, 1))
             fetch("x", xs)
-            fetch("sign", signs)
+            fetch("sign", signs - min(signs, 1))
             if pair == 7:
                 second_matmul(0, pair)
             for token_tile, path in products:

@@ -26,10 +26,6 @@ HALF = 512
 FLOPS = 2 * (2 * TOKENS * IN_F * RANK + 2 * TOKENS * RANK * OUT_F)
 
 
-def as_words(grouped, b):
-    return grouped[:, 1024 * b : 1024 * (b + 1)].rearrange("p (n u e) -> p n u e", u=2, e=2)
-
-
 def tile_littlebititqspeclinear_pa_kernel(
     tc, x, V, U, v2, v1, u2, u1, V_R, U_R, v2_R, v1_R, u2_R, u1_R, bias, out
 ):
@@ -82,57 +78,70 @@ def tile_littlebititqspeclinear_pa_kernel(
         ident_bf16 = consts.tile([P, P], BF16)
         make_identity(nc, ident_bf16[:])
 
-        def load_columns(rows, parts, which):
-            tiles = []
-            for i in which:
-                columns = IN_F // parts
-                raw = raws.tile([P, 2 * columns], BF16, name="raw%d" % parts, tag="raw%d" % parts, bufs=8 if parts == 4 else 10)
-                nc.sync.dma_start(
-                    out=raw[:].rearrange("p (s k) -> p s k", s=2), in_=rows[:, :, i * columns : (i + 1) * columns]
-                )
-                tiles.append(raw)
-            return tiles
+        def load(view, columns):
+            name = "raw%d" % (columns // 1024)
+            raw = raws.tile([P, columns], BF16, name=name, tag=name, bufs=8 if columns == 1024 else 10)
+            nc.sync.dma_start(out=raw[:].rearrange("p (s k) -> p s k", s=view.shape[1]), in_=view)
+            return raw
+
 
         def transposed_bank(psum, unit, b):
-            per_tile = len(unit["raw"])
-            words = unit["raw"][b * per_tile // 4][:].bitcast(F32)
-            local = b % (4 // per_tile)
             bank = psum.tile([P, BANK], F32, tag="bank")
             for u in range(2):
-                for s in range(2):
-                    first = local * unit["bank_step"] + s * (unit["block_step"] // per_tile) + P * u
+                for i in range(2):
+                    first, raw = unit["words"](b, u, i)
                     nc.tensor.transpose(
-                        bank[:, 256 * u + P * s : 256 * u + P * (s + 1)], words[:, first : first + P], ident[:]
+                        bank[:, 256 * u + P * i : 256 * u + P * (i + 1)], raw[:].bitcast(F32)[:, first : first + P], ident[:]
                     )
-            return bank[:].bitcast(BF16).rearrange("p (u n e) -> p n u e", u=2, e=2)
+            return bank[:].bitcast(BF16).rearrange("p (u i n e) -> p i n u e", u=2, i=2, e=2)
 
-        def open_v(path, pair, halves=(0, 1)):
+        def of_pass(tile, b):
+            return tile[:, 1024 * b : 1024 * (b + 1)].rearrange("p (i n u e) -> p i n u e", i=2, u=2, e=2)
+
+        def of_block(tile, b):
+            by_block = tile[:].rearrange("p (c s n u e) -> p c s n u e", c=IN_PASSES, s=2, u=2, e=2)
+            return by_block[:, 2 * (b % 2) : 2 * (b % 2) + 2, b // 2]
+
+        def open_v(path, pair, quarters=False):
             rows = (V, V_R)[path][256 * pair : 256 * (pair + 1), :].rearrange("(j s) k -> j s k", s=2)
-            return {
-                "raw": load_columns(rows, 2, halves), "rows": rows, "bank_step": 256, "block_step": 1024,
+            unit = {
+                "part": of_block, "rows": rows, "raw": [],
                 "codes": v_codes[path], "scales": v_scales[path], "first": UNIT_WORDS * pair,
             }
+            if quarters:
+                unit["words"] = lambda b, u, i: (256 * i + P * u, unit["raw"][b])
+            else:
+                unit["raw"] = [load(rows[:, s : s + 1, :], IN_F) for s in range(2)]
+                unit["words"] = lambda b, u, i: (512 * (b % 2) + 256 * i + P * u, unit["raw"][b // 2])
+            return unit
 
         def open_u(group):
-            tiles = []
-            for matrix in (U, U_R):
-                raw = raws.tile([P, 2 * IN_F // 2], BF16, name="raw2", tag="raw2", bufs=10)
-                nc.sync.dma_start(
-                    out=raw[:].rearrange("p (a r) -> p a r", r=RANK),
-                    in_=matrix[512 * group : 512 * (group + 1), :].rearrange("(a j) r -> j a r", j=P),
-                )
-                tiles.append(raw)
-            return {
-                "raw": tiles, "bank_step": 512, "block_step": 512,
-                "codes": u_codes, "scales": u_scales, "first": UNIT_WORDS * group,
-            }
+            unit = {"part": of_pass, "codes": u_codes, "scales": u_scales, "first": UNIT_WORDS * group}
+            unit["raw"] = [
+                load(matrix[512 * group : 512 * (group + 1), :].rearrange("(a j) r -> j a r", j=P), IN_F) for matrix in (U, U_R)
+            ]
+            unit["words"] = lambda b, u, i: (512 * (b % 2) + 256 * i + P * u, unit["raw"][b // 2])
+            return unit
 
-        def open_x(pair, halves=(0, 1)):
+        def open_x(pair, quarters=False):
             rows = x2[256 * pair : 256 * (pair + 1), :].rearrange("(s p) k -> p s k", p=P)
-            return {
-                "raw": load_columns(rows, 2, halves), "rows": rows, "bank_step": 256, "block_step": 1024,
-                "first": UNIT_WORDS * pair,
-            }
+            unit = {"part": of_pass, "rows": rows, "raw": [], "first": UNIT_WORDS * pair}
+            if quarters:
+                unit["words"] = lambda b, u, i: (256 * i + P * u, unit["raw"][b])
+            elif pair in (1,):
+                unit["raw"] = [load(rows[:, :, 1024 * h : 1024 * (h + 1)], IN_F) for h in range(2)]
+                unit["words"] = lambda b, u, i: (512 * i + 256 * (b % 2) + P * u, unit["raw"][b // 2])
+            else:
+                unit["raw"] = [load(rows[:, s : s + 1, :], IN_F) for s in range(2)]
+                unit["words"] = lambda b, u, i: (256 * b + P * u, unit["raw"][i])
+            return unit
+
+        def load_quarter(unit, b):
+            if unit["part"] == of_pass:
+                unit["raw"].append(load(unit["rows"][:, :, K_PASS * b : K_PASS * (b + 1)], 1024))
+            else:
+                half = slice(1024 * (b % 2), 1024 * (b % 2 + 1))
+                unit["raw"].append(load(unit["rows"][:, b // 2 : b // 2 + 1, half], 1024))
 
         banks, fetched, copied = {}, {"sign": 0, "x": 0}, {"sign": 0, "x": 0}
 
@@ -153,7 +162,7 @@ def tile_littlebititqspeclinear_pa_kernel(
                 unit, b, values = next_bank("sign")
                 if b == 0:
                     unit["signs"] = groups.tile([P, UNIT], BF16, name="signs", tag="signs", bufs=3, align_bytes=64)
-                nc.scalar.activation(out=as_words(unit["signs"], b), in_=values, func=ACT.Sign)
+                nc.scalar.activation(out=unit["part"](unit["signs"], b), in_=values, func=ACT.Sign)
 
         def close_signs(unit):
             quantise(unit["signs"], unit["codes"], unit["scales"], unit["first"], UNIT_WORDS)
@@ -168,8 +177,8 @@ def tile_littlebititqspeclinear_pa_kernel(
             for path in range(2):
                 v2_of_pass = by_k[:, v2_cols[path] + 4 * b : v2_cols[path] + 4 * (b + 1)]
                 nc.vector.tensor_tensor(
-                    out=as_words(unit["scaled"][path], b),
-                    in0=values,
+                    out=unit["part"](unit["scaled"][path], b).rearrange("p i n u e -> p (i n) u e"),
+                    in0=values.rearrange("p i n u e -> p (i n) u e"),
                     in1=v2_of_pass.rearrange("p (u e) -> p u e", u=2).unsqueeze(1).to_broadcast([P, 256, 2, 2]),
                     op=ALU.mult,
                 )
@@ -325,11 +334,11 @@ def tile_littlebititqspeclinear_pa_kernel(
             )
 
         ctx.enter_context(tc.manual_schedule())
-        x_units = [open_x(0, ())]
-        v_units = [open_v(0, 0, ())]
-        for i in range(4):
-            for unit in (x_units[0], v_units[0]):
-                unit["raw"].extend(load_columns(unit["rows"], 4, (i,)))
+        x_units = [open_x(0, True)]
+        v_units = [open_v(0, 0, True)]
+        for b in range(4):
+            load_quarter(x_units[0], b)
+            load_quarter(v_units[0], b)
         v_units.append(open_v(0, 1))
         x_units.append(open_x(1))
         v_units.extend([open_v(1, 0), open_v(1, 1)])

@@ -429,10 +429,10 @@ def tile_littlebititqspeclinear_pa_kernel(
         close_signs(v_units[3])
         x_bank()
         sign_bank()
-        fetch("x")
         fetch("sign")
         first_matmul(0, 1)
         first_matmul(1, 1)
+        fetch("x")
         close_h(0, 0)
         x_bank()
         sign_bank()
@@ -440,12 +440,11 @@ def tile_littlebititqspeclinear_pa_kernel(
         scale_h(0, 1)
         scale_h(1, 1)
         sign_bank()
-        fetch("sign")
+        fetch("sign", 2)
         first_matmul(2, 1)
         first_matmul(3, 1)
         x_bank()
         sign_bank()
-        fetch("sign")
         fetch("x")
         close_signs(u_units[0])
         scale_h(2, 1)

from contextlib import ExitStack

import concourse.mybir as mybir
from concourse.masks import make_identity

F32 = mybir.dt.float32
BF16 = mybir.dt.bfloat16
U32 = mybir.dt.uint32
U8 = mybir.dt.uint8
FP8X4 = mybir.dt.float8_e4m3fn_x4
ACT = mybir.ActivationFunctionType
ALU = mybir.AluOpType

P = 128
BANK = 512
K_PASS = 512
TOKENS = 1024
IN_F = 2048
RANK = 512
OUT_F = 2048
IN_PASSES = IN_F // K_PASS
UNIT = 4096
UNIT_WORDS = UNIT // 4
HALF = 512

FLOPS = 2 * (2 * TOKENS * IN_F * RANK + 2 * TOKENS * RANK * OUT_F)


def tile_littlebititqspeclinear_pa_kernel(
    tc, x, V, U, v2, v1, u2, u1, V_R, U_R, v2_R, v1_R, u2_R, u1_R, bias, out
):
    nc = tc.nc
    x2 = x.flatten_outer_dims()
    out2 = out.flatten_outer_dims()
    with ExitStack() as ctx:
        consts = ctx.enter_context(tc.tile_pool(name="consts", bufs=1))
        keep = ctx.enter_context(tc.tile_pool(name="keep", bufs=1))
        raws = ctx.enter_context(tc.tile_pool(name="raws", bufs=10))
        groups = ctx.enter_context(tc.tile_pool(name="groups", bufs=1))
        results = ctx.enter_context(tc.tile_pool(name="results", bufs=4))
        psum_s = ctx.enter_context(tc.psum_pool(name="psum_s", bufs=4))
        psum_v = ctx.enter_context(tc.psum_pool(name="psum_v", bufs=4))

        def mx_operand(name, columns):
            codes = [keep.tile([P, columns], U32, name="%s_codes%d" % (name, i), align_bytes=64) for i in range(2)]
            scales = [keep.tile([P, columns], U8, name="%s_scales%d" % (name, i), align_bytes=64) for i in range(2)]
            return codes, scales

        x_codes, x_scales = mx_operand("x", IN_PASSES * TOKENS)
        v_codes, v_scales = mx_operand("v", IN_PASSES * RANK)
        u_codes = keep.tile([P, 2 * OUT_F], U32, align_bytes=64)
        u_scales = keep.tile([P, 2 * OUT_F], U8, align_bytes=64)
        h_codes, h_scales = mx_operand("h", TOKENS)

        def quantise(grouped, codes, scales, first, columns):
            nc.vector.quantize_mx(
                out=codes[:, first : first + columns].bitcast(FP8X4),
                scales=scales[:, first : first + columns],
                in_=grouped[:],
            )

        def rows_of_256(queue, zeroing, vectors, name):
            rows_tile = consts.tile([P, 256], BF16, name=name)
            zeroing.memset(rows_tile[:], 0.0)
            first_row = 0
            for vec in vectors:
                rows = vec.shape[1] // 256
                queue.dma_start(
                    out=rows_tile[first_row : first_row + rows, :], in_=vec.rearrange("o (r c) -> (o r) c", c=256)
                )
                first_row += rows
            return rows_tile

        v2_rows = rows_of_256(nc.sync, nc.gpsimd, (v2, v2_R), "v2_rows")

        ident = consts.tile([P, P], F32)
        make_identity(nc, ident[:])
        ident_bf16 = consts.tile([P, P], BF16)
        make_identity(nc, ident_bf16[:])

        def load(view, columns):
            name = "raw%d" % (columns // 1024)
            raw = raws.tile([P, columns], BF16, name=name, tag=name, bufs=8 if columns == 1024 else 10)
            nc.sync.dma_start(out=raw[:].rearrange("p (s k) -> p s k", s=view.shape[1]), in_=view)
            return raw


        def transposed_bank(psum, unit, b):
            bank = psum.tile([P, BANK], F32, tag="bank")
            for u in range(2):
                for i in range(2):
                    first, raw = unit["words"](b, u, i)
                    nc.tensor.transpose(
                        bank[:, 256 * u + P * i : 256 * u + P * (i + 1)], raw[:].bitcast(F32)[:, first : first + P], ident[:]
                    )
            return bank[:].bitcast(BF16).rearrange("p (u i n e) -> p i n u e", u=2, i=2, e=2)

        def of_pass(tile, b):
            return tile[:, 1024 * b : 1024 * (b + 1)].rearrange("p (i n u e) -> p i n u e", i=2, u=2, e=2)

        def of_block(tile, b):
            by_block = tile[:].rearrange("p (c s n u e) -> p c s n u e", c=IN_PASSES, s=2, u=2, e=2)
            return by_block[:, 2 * (b % 2) : 2 * (b % 2) + 2, b // 2]

        def open_v(path, pair, quarters=False):
            rows = (V, V_R)[path][256 * pair : 256 * (pair + 1), :].rearrange("(j s) k -> j s k", s=2)
            unit = {
                "part": of_block, "rows": rows, "raw": [],
                "codes": v_codes[path], "scales": v_scales[path], "first": UNIT_WORDS * pair,
            }
            if quarters:
                unit["words"] = lambda b, u, i: (256 * i + P * u, unit["raw"][b])
            else:
                unit["raw"] = [load(rows[:, s : s + 1, :], IN_F) for s in range(2)]
                unit["words"] = lambda b, u, i: (512 * (b % 2) + 256 * i + P * u, unit["raw"][b // 2])
            return unit

        def open_u(group):
            unit = {"part": of_pass, "codes": u_codes, "scales": u_scales, "first": UNIT_WORDS * group}
            unit["raw"] = [
                load(matrix[512 * group : 512 * (group + 1), :].rearrange("(a j) r -> j a r", j=P), IN_F) for matrix in (U, U_R)
            ]
            unit["words"] = lambda b, u, i: (512 * (b % 2) + 256 * i + P * u, unit["raw"][b // 2])
            return unit

        def open_x(pair, quarters=False):
            rows = x2[256 * pair : 256 * (pair + 1), :].rearrange("(s p) k -> p s k", p=P)
            unit = {"part": of_pass, "rows": rows, "raw": [], "first": UNIT_WORDS * pair}
            if quarters:
                unit["words"] = lambda b, u, i: (256 * i + P * u, unit["raw"][b])
            elif pair in (1,):
                unit["raw"] = [load(rows[:, :, 1024 * h : 1024 * (h + 1)], IN_F) for h in range(2)]
                unit["words"] = lambda b, u, i: (512 * i + 256 * (b % 2) + P * u, unit["raw"][b // 2])
            else:
                unit["raw"] = [load(rows[:, s : s + 1, :], IN_F) for s in range(2)]
                unit["words"] = lambda b, u, i: (256 * b + P * u, unit["raw"][i])
            return unit

        def load_quarter(unit, b):
            if unit["part"] == of_pass:
                unit["raw"].append(load(unit["rows"][:, :, K_PASS * b : K_PASS * (b + 1)], 1024))
            else:
                half = slice(1024 * (b % 2), 1024 * (b % 2 + 1))
                unit["raw"].append(load(unit["rows"][:, b // 2 : b // 2 + 1, half], 1024))

        banks, fetched, copied = {}, {"sign": 0, "x": 0}, {"sign": 0, "x": 0}

        def fetch(stream, count=1):
            for unit, b in streams[stream][fetched[stream] : fetched[stream] + count]:
                psum = psum_s if stream == "sign" else psum_v
                banks[(stream, fetched[stream])] = (unit, b, transposed_bank(psum, unit, b))
                fetched[stream] += 1

        def next_bank(stream):
            if copied[stream] == fetched[stream]:
                fetch(stream)
            copied[stream] += 1
            return banks[(stream, copied[stream] - 1)]

        def sign_bank(count=1):
            for i in range(count):
                unit, b, values = next_bank("sign")
                if b == 0:
                    unit["signs"] = groups.tile([P, UNIT], BF16, name="signs", tag="signs", bufs=3, align_bytes=64)
                nc.scalar.activation(out=unit["part"](unit["signs"], b), in_=values, func=ACT.Sign)

        def close_signs(unit):
            quantise(unit["signs"], unit["codes"], unit["scales"], unit["first"], UNIT_WORDS)

        def x_bank():
            unit, b, values = next_bank("x")
            if b == 0:
                unit["scaled"] = [
                    groups.tile([P, UNIT], BF16, name="scaled%d" % path, tag="scaled%d" % path, align_bytes=64)
                    for path in range(2)
                ]
            for path in range(2):
                v2_of_pass = by_k[:, v2_cols[path] + 4 * b : v2_cols[path] + 4 * (b + 1)]
                nc.vector.tensor_tensor(
                    out=unit["part"](unit["scaled"][path], b).rearrange("p i n u e -> p (i n) u e"),
                    in0=values.rearrange("p i n u e -> p (i n) u e"),
                    in1=v2_of_pass.rearrange("p (u e) -> p u e", u=2).unsqueeze(1).to_broadcast([P, 256, 2, 2]),
                    op=ALU.mult,
                )

        def close_x(unit, paths=(0, 1)):
            for path in paths:
                quantise(unit["scaled"][path], x_codes[path], x_scales[path], unit["first"], UNIT_WORDS)

        h_scaled = [None, None]

        h_banks = {}

        def first_matmul(token_tile, path):
            tokens = UNIT_WORDS * (token_tile // 2) + P * (token_tile % 2)
            h_bank = psum_v.tile([P, BANK], F32, tag="bank")
            for t in range(4):
                ranks = UNIT_WORDS * (t // 2) + P * (t % 2)
                for c in range(IN_PASSES):
                    nc.tensor.matmul_mx(
                        out=h_bank[:, P * t : P * (t + 1)],
                        lhsT=v_codes[path][:, ranks + 256 * c : ranks + 256 * c + P].bitcast(FP8X4),
                        lhsT_scale=v_scales[path][:, ranks + 256 * c : ranks + 256 * c + P],
                        rhs=x_codes[path][:, tokens + 256 * c : tokens + 256 * c + P].bitcast(FP8X4),
                        rhs_scale=x_scales[path][:, tokens + 256 * c : tokens + 256 * c + P],
                        start=(c == 0),
                        stop=(c == IN_PASSES - 1),
                    )
            h_banks[(token_tile, path)] = h_bank

        def scale_h(token_tile, path):
            i = token_tile % (HALF // P)
            if i == 0:
                h_scaled[path] = groups.tile(
                    [P, 4 * HALF], BF16, name="h_scaled%d" % path, tag="h_scaled%d" % path, align_bytes=64
                )
            nc.vector.tensor_tensor(
                out=h_scaled[path][:, 4 * P * i : 4 * P * (i + 1)].rearrange("p (n t) -> p n t", t=4),
                in0=h_banks[(token_tile, path)][:].rearrange("p (t n) -> p n t", t=4),
                in1=rank_scale[:, path, :].unsqueeze(1).to_broadcast([P, P, 4]),
                op=ALU.mult,
            )

        def close_h(path, half):
            quantise(h_scaled[path], h_codes[path], h_scales[path], HALF * half, HALF)

        accs, primaries, sums, y_banks = {}, {}, {}, {}
        added_in_psum = [(0, 1), (0, 3), (0, 15)]

        def second_matmul(half, pair):
            tokens = slice(HALF * half, HALF * (half + 1))
            for a in (2 * pair, 2 * pair + 1):
                for path in range(2):
                    acc = (psum_s, psum_v)[path].tile([P, BANK], F32, tag="bank", name="acc%d" % path)
                    first = UNIT_WORDS * (a // 4) + 4 * P * path + P * (a % 4)
                    nc.tensor.matmul_mx(
                        out=acc[:],
                        lhsT=u_codes[:, first : first + P].bitcast(FP8X4),
                        lhsT_scale=u_scales[:, first : first + P],
                        rhs=h_codes[path][:, tokens].bitcast(FP8X4),
                        rhs_scale=h_scales[path][:, tokens],
                        start=True,
                        stop=True,
                    )
                    accs[(half, a, path)] = acc

        def scale_primary(half, pair):
            for a in (2 * pair, 2 * pair + 1):
                primary = results.tile([P, HALF], F32, tag="primary")
                nc.scalar.activation(
                    out=primary[:],
                    in_=accs[(half, a, 0)][:],
                    func=ACT.Identity,
                    scale=by_o[:, a : a + 1],
                    bias=by_o[:, 2 * o_tiles + a : 2 * o_tiles + a + 1],
                )
                primaries[(half, a)] = primary
                if (half, a) in added_in_psum:
                    residual = results.tile([P, HALF], F32, tag="residual", bufs=2)
                    nc.scalar.activation(
                        out=residual[:], in_=accs[(half, a, 1)][:], func=ACT.Copy, scale=by_o[:, o_tiles + a : o_tiles + a + 1]
                    )
                    sums[(half, a)] = residual

        def add_residual(half, pair):
            for a in (2 * pair, 2 * pair + 1):
                if (half, a) in added_in_psum:
                    continue
                both = results.tile([P, HALF], F32, tag="both", bufs=5)
                nc.vector.scalar_tensor_tensor(
                    out=both[:],
                    in0=accs[(half, a, 1)][:],
                    scalar=by_o[:, o_tiles + a : o_tiles + a + 1],
                    in1=primaries[(half, a)][:],
                    op0=ALU.mult,
                    op1=ALU.add,
                )
                sums[(half, a)] = both

        def transpose_back(half, pair, split, parts=1):
            tiles = HALF // P // parts
            for j in range(2):
                y_banks[(half, pair, j)] = []
                a = 2 * pair + j
                terms = (primaries[(half, a)], sums[(half, a)]) if (half, a) in added_in_psum else (sums[(half, a)],)
                for i in range(HALF // P):
                    if i % tiles == 0:
                        y_bank = (psum_v if split and j == 1 else psum_s).tile([P, BANK], F32, tag="bank", name="y_bank")
                        y_banks[(half, pair, j)].append(y_bank)
                    for n, term in enumerate(terms):
                        nc.tensor.matmul(
                            y_bank[:, P * (i % tiles) : P * (i % tiles + 1)],
                            lhsT=term[:, P * i : P * (i + 1)],
                            rhs=ident[:],
                            is_transpose=True,
                            start=(n == 0),
                            stop=(n == len(terms) - 1),
                        )

        def store(half, pair, split, parts=1):
            tiles = HALF // P // parts
            for part in range(parts):
                if parts == 1:
                    y = raws.tile([P, tiles, 2 * P], F32, name="y", tag="raw2", bufs=10)
                else:
                    y = results.tile([P, tiles, 2 * P], F32, name="y_part", tag="y_part", bufs=4)
                for j in range(2):
                    banks = y_banks[(half, pair, j)]
                    bank, offset = divmod(HALF * part // parts, HALF // len(banks))
                    by_tile = banks[bank][:, offset : offset + P * tiles].rearrange("p (i f) -> p i f", f=P)
                    if split and j == 1:
                        nc.vector.tensor_copy(out=y[:, :, P * j : P * (j + 1)], in_=by_tile)
                    else:
                        nc.scalar.copy(out=y[:, :, P * j : P * (j + 1)], in_=by_tile)
                first = HALF * half + P * tiles * part
                nc.sync.dma_start(
                    out=out2[first : first + P * tiles, 2 * P * pair : 2 * P * (pair + 1)].rearrange(
                        "(i p) f -> p i f", p=P
                    ),
                    in_=y[:],
                )

        scratch = consts.tile([P, 1], F32)
        nc.vector.memset(scratch[:], 0.0)
        nc.scalar.activation(out=scratch[:], in_=scratch[:], func=ACT.Sign)

        rank_rows = rows_of_256(nc.scalar, nc.vector, (v1, u2, v1_R, u2_R), "rank_rows")
        by_o_rows = consts.tile([P, P], BF16)
        nc.vector.memset(by_o_rows[:], 0.0)
        o_tiles = OUT_F // P
        for i, vec in enumerate((u1.rearrange("o f -> (o f)"), u1_R.rearrange("o f -> (o f)"), bias)):
            nc.scalar.dma_start(
                out=by_o_rows[o_tiles * i : o_tiles * (i + 1), :], in_=vec.rearrange("(r c) -> r c", c=P)
            )

        ctx.enter_context(tc.manual_schedule())
        x_units = [open_x(0, True)]
        v_units = [open_v(0, 0, True)]
        for b in range(4):
            load_quarter(x_units[0], b)
            load_quarter(v_units[0], b)
        v_units.append(open_v(0, 1))
        x_units.append(open_x(1))
        v_units.extend([open_v(1, 0), open_v(1, 1)])
        u_units = [open_u(0)]
        x_units.append(open_x(2))
        u_units.append(open_u(1))
        x_units.append(open_x(3))
        u_units.extend([open_u(2), open_u(3)])
        streams = {
            "sign": [(unit, b) for unit in v_units + u_units for b in range(4)],
            "x": [(unit, b) for unit in x_units for b in range(4)],
        }

        def word_transpose(rows_tile, name):
            bank = psum_v.tile([P, BANK], F32, tag="bank", name=name)
            nc.tensor.transpose(bank[:, 0:P], rows_tile[:].bitcast(F32), ident[:])
            return bank

        def table(copy, bank, columns, name):
            values = consts.tile([P, columns], BF16, name=name)
            copy(out=values[:], in_=bank[:].bitcast(BF16)[:, 0:columns])
            return values

        by_k = table(nc.vector.tensor_copy, word_transpose(v2_rows, "by_k_bank"), 32, "by_k")
        fetch("x")
        v2_cols = (0, 16)
        for b in range(4):
            x_bank()
            sign_bank()
        fetch("sign")
        close_x(x_units[0], (0,))
        sign_bank()
        fetch("sign")
        close_x(x_units[0], (1,))
        close_signs(v_units[0])
        sign_bank()

        for i in range(2):
            fetch("sign")
            fetch("x", 1 + i)
            x_bank()
            sign_bank()
        fetch("sign")
        fetch("x")
        sign_bank()
        fetch("sign")
        close_signs(v_units[1])
        x_bank()
        sign_bank()
        x_bank()
        for i in range(2):
            fetch("sign")
            sign_bank()
        by_rank_bank = word_transpose(rank_rows, "by_rank_bank")
        by_rank = table(nc.scalar.copy, by_rank_bank, 16, "by_rank")
        rank_scale = consts.tile([P, 2, 4], F32)
        by_path = by_rank[:].rearrange("p (q w t) -> p q w t", q=2, w=2)
        nc.gpsimd.tensor_tensor(out=rank_scale[:], in0=by_path[:, :, 0, :], in1=by_path[:, :, 1, :], op=ALU.mult)
        first_matmul(0, 0)
        fetch("sign", 2)
        first_matmul(1, 0)
        close_x(x_units[1], (0,))
        sign_bank()
        fetch("sign")
        close_x(x_units[1], (1,))
        sign_bank()
        by_o_bank = psum_v.tile([P, BANK], F32, tag="bank")
        nc.tensor.transpose(by_o_bank[:].bitcast(BF16)[:, 0:P], by_o_rows[:], ident_bf16[:])
        by_o = consts.tile([P, 3 * o_tiles], F32)
        nc.scalar.copy(out=by_o[:], in_=by_o_bank[:].bitcast(BF16)[:, 0 : 3 * o_tiles])
        fetch("sign")
        first_matmul(2, 0)
        first_matmul(3, 0)
        scale_h(0, 0)
        scale_h(1, 0)
        sign_bank()
        close_signs(v_units[2])
        sign_bank()
        fetch("sign")
        fetch("x", 2)
        fetch("sign")
        sign_bank()
        fetch("sign")
        scale_h(2, 0)
        scale_h(3, 0)
        sign_bank()
        fetch("sign")
        close_signs(v_units[3])
        x_bank()
        sign_bank()
        fetch("sign")
        first_matmul(0, 1)
        first_matmul(1, 1)
        fetch("x")
        close_h(0, 0)
        x_bank()
        sign_bank()
        fetch("sign")
        scale_h(0, 1)
        scale_h(1, 1)
        sign_bank()
        fetch("sign", 2)
        first_matmul(2, 1)
        first_matmul(3, 1)
        x_bank()
        sign_bank()
        fetch("x")
        close_signs(u_units[0])
        scale_h(2, 1)
        scale_h(3, 1)
        close_h(1, 0)
        sign_bank()
        x_bank()
        sign_bank()
        fetch("sign")

        def step(pair, signs, xs, products, vector_work, vector_work_after=()):
            fetch("sign", min(signs, 1))
            fetch("x", xs)
            fetch("sign", signs - min(signs, 1))
            if pair == 7:
                second_matmul(0, pair)
            for token_tile, path in products:
                first_matmul(token_tile, path)
            if pair < 7:
                second_matmul(0, pair)
            if pair > 0:
                transpose_back(0, pair - 1, False)
            sign_bank(signs)
            scale_primary(0, pair)
            for work in vector_work:
                work()
            add_residual(0, pair)
            for work in vector_work_after:
                work()
            if pair > 0:
                store(0, pair - 1, False)

        step(0, 1, 0, (), (lambda: close_x(x_units[2]),))
        step(1, 3, 1, ((4, 0), (4, 1)), (x_bank, lambda: close_signs(u_units[1])), (lambda: scale_h(4, 0), lambda: scale_h(4, 1)))
        step(2, 2, 3, ((5, 0),), (x_bank, x_bank, x_bank), (lambda: scale_h(5, 0),))
        step(
            3, 1, 0, ((5, 1),),
            (lambda: close_x(x_units[3], (0,)), lambda: close_signs(u_units[2])), (lambda: scale_h(5, 1),),
        )
        step(4, 0, 0, ((6, 0),), (lambda: scale_h(6, 0),), (lambda: close_x(x_units[3], (1,)),))
        step(5, 1, 0, ((7, 0),), (lambda: close_signs(u_units[3]),))
        step(6, 0, 0, ((6, 1),), (lambda: scale_h(7, 0),))
        step(7, 0, 0, ((7, 1),), (lambda: close_h(0, 1), lambda: scale_h(6, 1)))
        scale_h(7, 1)
        close_h(1, 1)
        transpose_back(0, 7, True)
        store(0, 7, True)

        for made, back in (((0, 1, 2), (0, 1)), ((3, 4), (2, 3)), ((5,), (4,)), ((6,), (5,)), ((7,), (6,))):
            for pair in made:
                second_matmul(1, pair)
            for pair in made:
                scale_primary(1, pair)
                add_residual(1, pair)
            for pair in back:
                transpose_back(1, pair, pair < 6)
            for pair in back:
                store(1, pair, pair < 6, 1 if pair < 6 else 2)
        transpose_back(1, 7, True, 2)
        store(1, 7, True, 2)
